import numpy as np
import ml_dtypes


def mxq(x, axis, fmt="e4m3"):
    dtype, down = {"e4m3": (ml_dtypes.float8_e4m3fn, 7), "e5m2": (ml_dtypes.float8_e5m2, 14)}[fmt]
    v = np.moveaxis(np.asarray(x, np.float32).astype(ml_dtypes.bfloat16).astype(np.float64), axis, -1)
    blocks = v.reshape(v.shape[:-1] + (-1, 32))
    amax = np.abs(blocks).max(-1, keepdims=True)
    byte = np.maximum(np.where(amax > 0, np.frexp(amax)[1] - 1 + 127, 0) - down, 1)
    scale = np.exp2(byte - 127.0)
    codes = (blocks / scale).astype(np.float32).astype(dtype).astype(np.float64)
    return np.moveaxis((codes * scale).reshape(v.shape), -1, axis)


WIDE = False


def mx_kscale(k):
    if not WIDE:
        return np.ones(k)
    levels = np.array([18, -18])
    if k % 512:
        return np.exp2(np.random.permutation(np.resize(levels, k // 32))).repeat(32)
    a = np.empty((k // 512, 16))
    for p in range(k // 512):
        a[p, :8] = np.random.permutation(np.resize(levels, 8))
        for g in range(8):
            far = levels[np.abs(levels - a[p, g]) >= 10]
            a[p, g + 8] = far[np.random.randint(len(far))]
    return np.exp2(a.ravel()).repeat(32)


BF16 = ml_dtypes.bfloat16


def bf(x):
    return np.asarray(x, np.float32).astype(BF16)


def f64(x):
    return np.asarray(x).astype(np.float64)


B, TQ, TV, H, DH = 1, 512, 1024, 4, 512
D = H * DH


def heads(a, n):
    return a.reshape(B, n, H, DH).transpose(0, 2, 1, 3)


def unheads(a, n):
    return a.transpose(0, 2, 1, 3).reshape(B, n, D)


def head_softmax(query, k):
    qk = (heads(f64(query), TQ) @ heads(f64(k), TV).transpose(0, 1, 3, 2)) * DH ** -0.5
    e = np.exp(qk - qk.max(axis=1, keepdims=True))
    return e / e.sum(axis=1, keepdims=True)


def setup_inputs():
    u = mx_kscale(DH)
    v = mx_kscale(TV)[:, None]
    s = mx_kscale(TQ)[:, None]
    q0 = bf(np.random.standard_normal((B, TQ, D)))
    k0 = bf(np.random.standard_normal((B, TV, D)))
    v0 = bf(np.random.standard_normal((B, TV, DH)) * 0.5)
    g = bf(np.random.standard_normal((B, TQ, D)) * np.exp2(np.random.randint(-6, 1, (B, TQ, 1))) / s * np.tile(u, H))
    w = head_softmax(q0, k0)
    return {"query": bf(f64(q0) * s), "k": bf(f64(k0) / v), "value": bf(f64(v0) * v / u),
            "w": np.asarray(w, np.float32), "grad_out": g}


def reference(query, k, value, w, grad_out):
    wf = f64(w)
    g = heads(f64(grad_out), TQ)
    vq = mxq(f64(value), 2, "e4m3").transpose(0, 2, 1)[:, None]
    dw = mxq(g, 3, "e5m2") @ vq
    ds = wf * (dw - (wf * dw).sum(axis=1, keepdims=True)) * DH ** -0.5
    dq = mxq(ds, 3, "e5m2") @ mxq(heads(f64(k), TV), 2, "e4m3")
    dk = mxq(ds, 2, "e5m2").transpose(0, 1, 3, 2) @ mxq(heads(f64(query), TQ), 2, "e4m3")
    return unheads(dq, TQ), unheads(dk, TV)

@@ -1,0 +1,353 @@
+from contextlib import ExitStack
+
+import concourse.mybir as mybir
+from concourse.masks import make_identity
+
+F32 = mybir.dt.float32
+BF16 = mybir.dt.bfloat16
+U32 = mybir.dt.uint32
+U8 = mybir.dt.uint8
+E4M3 = mybir.dt.float8_e4m3fn_x4
+E5M2 = mybir.dt.float8_e5m2_x4
+ALU = mybir.AluOpType
+
+P = 128
+PACK = 4
+PASS = P * PACK
+TQ, TV, H, DH = 512, 1024, 4, 512
+HALVES = TV // PASS
+SCALE = DH ** -0.5
+FLOPS = 3 * 2 * H * TQ * TV * DH
+
+
+def tile_multiheadattention_pa_v_kernel(tc, query, k, value, w, grad_out, out_0, out_1):
+    nc = tc.nc
+    q_rows = query.rearrange("b (p j) d -> p (b j) d", j=PACK)
+    g_rows = grad_out.rearrange("b (p j) d -> p (b j) d", j=PACK)
+    k_rows = k.rearrange("b (g m s) d -> m (b g) s d", g=HALVES, s=PACK)
+    v_rows = value.rearrange("b (g m s) d -> m (b g) s d", g=HALVES, s=PACK)
+    w_rows = w.rearrange("b h (p j) t -> p (b h) j t", j=PACK)
+    dq_rows = out_0.rearrange("b (p j) d -> p (b j) d", j=PACK)
+    dk_rows = out_1.rearrange("b (g m s) d -> m (b g) s d", g=HALVES, s=PACK)
+
+    with ExitStack() as ctx:
+        sb = ctx.enter_context(tc.tile_pool(name="sb", bufs=1))
+        ps = ctx.enter_context(tc.psum_pool(name="ps", bufs=1))
+
+        def bank(i):
+            return ps.tile([P, PASS], F32, name="bank%d" % i, tag="bank%d" % i)
+
+        def copy(engine, out, in_):
+            if engine == "s":
+                nc.scalar.copy(out=out, in_=in_)
+            else:
+                nc.vector.tensor_copy(out=out, in_=in_)
+
+        def staged(tag, bufs):
+            return sb.tile([P, PACK * PASS], BF16, name=tag, tag=tag, bufs=bufs, align_bytes=64)
+
+        mx = {}
+
+        def quantise(key, values, fmt, tag, bufs):
+            width = values.shape[1] // PACK
+            codes = sb.tile([P, width], U32, name=tag + "_codes", tag=tag + "_codes", bufs=bufs, align_bytes=64)
+            scales = sb.tile([P, width], U8, name=tag + "_scales", tag=tag + "_scales", bufs=bufs, align_bytes=64)
+            nc.vector.quantize_mx(out=codes[:].bitcast(fmt), scales=scales[:], in_=values)
+            mx[key] = (codes, scales, fmt)
+
+        def mx_pass(acc, stationary, block, moving, start, stop):
+            s_codes, s_scales, s_fmt = mx[stationary]
+            m_codes, m_scales, m_fmt = mx[moving]
+            cols = slice(block * P, (block + 1) * P)
+            nc.tensor.matmul_mx(
+                out=acc[:],
+                lhsT=s_codes[:, cols].bitcast(s_fmt),
+                lhsT_scale=s_scales[:, cols],
+                rhs=m_codes[:].bitcast(m_fmt),
+                rhs_scale=m_scales[:],
+                start=start,
+                stop=stop,
+            )
+
+        raw = {}
+
+        def io_tile(shape, dtype):
+            return sb.tile(shape, dtype, name="io", tag="io", bufs=5, align_bytes=64)
+
+        def load_v(g):
+            raw["v", g] = io_tile([P, PACK, DH], BF16)
+            nc.sync.dma_start(out=raw["v", g][:], in_=v_rows[:, g])
+
+        def load_g(j):
+            raw["g", j] = io_tile([P, H * DH], BF16)
+            nc.sync.dma_start(out=raw["g", j][:], in_=g_rows[:, j])
+
+        def load_pair(key, rows, pair):
+            raw[key, pair] = sb.tile([P, PACK, 2 * DH], BF16, name="pair", tag="pair", bufs=4, align_bytes=64)
+            nc.sync.dma_start(out=raw[key, pair][:], in_=rows[:, :, 2 * DH * pair : 2 * DH * (pair + 1)])
+
+        wt = {}
+
+        def load_w(g, h, j0, j1):
+            if j0 == 0:
+                wt[g, h] = sb.tile([P, PACK, PASS], F32, name="wt", tag="wt", bufs=6, align_bytes=64)
+            nc.sync.dma_start(out=wt[g, h][:, j0:j1, :], in_=w_rows[:, h, j0:j1, PASS * g : PASS * (g + 1)])
+
+        ident = sb.tile([P, P], F32, name="ident", align_bytes=64)
+        grouped = {}
+
+        def turn(key, banks, engines):
+            words = raw[key][:].bitcast(F32) if key[0] == "g" else raw[key][:].rearrange("p b d -> p (b d)").bitcast(F32)
+            grouped[key] = staged("grouped", 3)
+            out_words = grouped[key][:].bitcast(F32)
+            for half in range(2):
+                xt = bank(banks[half])
+                for i in range(4):
+                    b, u = 2 * half + i // 2, i % 2
+                    nc.tensor.transpose(xt[:, i * P : (i + 1) * P], words[:, 256 * b + u : 256 * (b + 1) : 2], ident[:])
+                src = xt[:].rearrange("x (b u r) -> x b r u", b=2, u=2)
+                if key[0] == "g":
+                    dst = out_words.rearrange("x (b r u) -> x b r u", b=4, u=2)[:, 2 * half : 2 * half + 2]
+                    copy(engines[half], dst, src)
+                else:
+                    dst = out_words.rearrange("x (r b u) -> x r b u", b=4, u=2)[:, :, 2 * half : 2 * half + 2]
+                    copy(engines[half], dst, xt[:].rearrange("x (b u r) -> x r b u", b=2, u=2))
+
+        def interleave(key, h, engines):
+            src = raw[key, h // 2][:, :, DH * (h % 2) : DH * (h % 2 + 1)].rearrange("p t (a c i) -> p a c t i", a=2, i=4)
+            grouped[key, h] = staged("grouped", 3)
+            dst = grouped[key, h][:].rearrange("p (a c i t) -> p a c t i", a=2, i=4, t=PACK)
+            for a in range(2):
+                copy(engines[a], dst[:, a], src[:, a])
+
+        def quantise_rows(key, h):
+            quantise((key, h), grouped[key, h][:], E4M3, "q" if key == "q" else "k", H if key == "q" else HALVES * H)
+
+        def quantise_g(j, pair):
+            quantise(("g", j, pair), grouped["g", j][:, 1024 * pair : 1024 * (pair + 1)], E5M2, "g", 2 * PACK)
+
+        def quantise_v(g):
+            quantise(("v", g), grouped["v", g][:], E4M3, "v", HALVES)
+
+        dw = {}
+        prod = {}
+        r = {}
+        r_turned = {}
+
+        def work_bank(g, i):
+            return bank(4 * (1 - g) + i % 4)
+
+        def r_bank(g, j):
+            return bank(4 * g + j)
+
+        def dw_pass(g, j, h):
+            dw[j, h] = work_bank(g, h)
+            mx_pass(dw[j, h], ("g", j, h // 2), h % 2, ("v", g), True, True)
+
+        def product(g, j, h):
+            if j == 0:
+                prod[h] = sb.tile([P, PACK, PASS], F32, name="prod", tag="prod", bufs=H, align_bytes=64)
+            nc.vector.scalar_tensor_tensor(
+                out=prod[h][:, j, :], in0=dw[j, h][:], scalar=SCALE, in1=wt[g, h][:, j, :], op0=ALU.mult, op1=ALU.mult
+            )
+
+        def head_sum(g, j):
+            acc = r_bank(g, j)
+            for b in range(4):
+                cols = slice(b * P, (b + 1) * P)
+                for h in range(H):
+                    nc.tensor.matmul(
+                        acc[:, cols], lhsT=prod[h][:, j, cols], rhs=ident[:], start=h == 0, stop=h == H - 1, is_transpose=True
+                    )
+            r_turned[j] = sb.tile([P, PASS], F32, name="r_turned", tag="r_turned", bufs=2, align_bytes=64)
+            nc.scalar.copy(out=r_turned[j][:], in_=acc[:])
+
+        def turn_back(g, j):
+            r[j] = r_bank(g, j)
+            for b in range(4):
+                cols = slice(b * P, (b + 1) * P)
+                nc.tensor.transpose(r[j][:, cols], r_turned[j][:, cols], ident[:])
+
+        ds_q = {}
+        ds_t = {}
+        used = {0: 0, 1: 0}
+
+        def next_bank(g):
+            used[g] = used[g] + 1
+            return work_bank(g, used[g] - 1)
+
+        def weighted_sum(g, h, j):
+            nc.vector.tensor_tensor(out=wt[g, h][:, j, :], in0=r[j][:], in1=wt[g, h][:, j, :], op=ALU.mult)
+
+        def finish_ds(g, h, u):
+            if u == 0:
+                ds_q[h] = staged("ds_q", 2)
+            view = "p j (m u e) -> p u m j e"
+            nc.vector.tensor_tensor(
+                out=ds_q[h][:].rearrange("p (u e m j) -> p u m j e", u=2, e=2, j=PACK)[:, u],
+                in0=prod[h][:].rearrange(view, u=2, e=2)[:, u],
+                in1=wt[g, h][:].rearrange(view, u=2, e=2)[:, u],
+                op=ALU.subtract,
+            )
+
+        def turn_ds(g, h, engines, bank_half):
+            words = ds_q[h][:].bitcast(F32)
+            ds_t[h] = staged("ds_t", 2)
+            xt = [next_bank(bank_half), next_bank(bank_half)]
+            for u in range(2):
+                for jj in range(2):
+                    for s in (2 * u, 2 * u + 1):
+                        nc.tensor.transpose(
+                            xt[jj][:, s * P : (s + 1) * P], words[:, 256 * s + jj : 256 * (s + 1) : 2], ident[:]
+                        )
+            for jj in range(2):
+                copy(
+                    engines[jj],
+                    ds_t[h][:, 1024 * jj : 1024 * (jj + 1)].rearrange("m (e p s) -> m e p s", e=2, s=PACK),
+                    xt[jj][:].bitcast(BF16).rearrange("m (s p e) -> m e p s", s=PACK, e=2),
+                )
+
+        def store(accs, rows, h, engines):
+            result = io_tile([P, 2, DH], F32)
+            for i in range(2):
+                copy(engines[i], result[:, i, :], accs[i][:])
+            nc.sync.dma_start(out=rows[:, :, DH * h : DH * (h + 1)], in_=result[:])
+
+        def grad_k_passes(g, h, pair, bank_half):
+            accs = []
+            for s in (2 * pair, 2 * pair + 1):
+                accs.append(next_bank(bank_half))
+                mx_pass(accs[-1], ("ds_q", g, h), s, ("q", h), True, True)
+            return accs, dk_rows[:, g, 2 * pair : 2 * pair + 2], h
+
+        def grad_q_passes(h, pair, bank_half):
+            accs = []
+            for j in (2 * pair, 2 * pair + 1):
+                accs.append(next_bank(bank_half))
+                for g in range(HALVES):
+                    mx_pass(accs[-1], ("ds_t", g, h, j // 2), j % 2, (("k", g), h), g == 0, g == HALVES - 1)
+            return accs, dq_rows[:, 2 * pair : 2 * pair + 2], h
+
+        def quantise_ds_q(g, h):
+            quantise(("ds_q", g, h), ds_q[h][:], E5M2, "ds_q", 4)
+
+        def quantise_ds_t(g, h):
+            for jj in range(2):
+                quantise(("ds_t", g, h, jj), ds_t[h][:, 1024 * jj : 1024 * (jj + 1)], E5M2, "ds_t", 2 * H + 4)
+
+        K0, K1 = ("k", 0), ("k", 1)
+        load_v(0)
+        load_g(0)
+        load_w(0, 0, 0, 2)
+        load_g(1)
+        load_w(0, 1, 0, 2)
+        load_w(0, 2, 0, 2)
+        load_w(0, 3, 0, 2)
+        load_g(2)
+        load_pair("q", q_rows, 0)
+        load_g(3)
+        for h in range(H):
+            load_w(0, h, 2, 4)
+        load_pair("q", q_rows, 1)
+        load_pair(K0, k_rows[:, 0], 0)
+        load_pair(K1, k_rows[:, 1], 0)
+        make_identity(nc, ident[:])
+
+        turn(("v", 0), (4, 5), "sv")
+        turn(("g", 0), (6, 7), "ss")
+        load_v(1)
+        load_w(1, 0, 0, 4)
+        load_w(1, 1, 0, 4)
+        quantise_v(0)
+        quantise_g(0, 0)
+        dw_pass(0, 0, 0)
+        dw_pass(0, 0, 1)
+        quantise_g(0, 1)
+        dw_pass(0, 0, 2)
+        dw_pass(0, 0, 3)
+        turn(("g", 1), (0, 1), "ss")
+
+        def rows_operand(key, h, engines):
+            interleave(key, h, engines)
+            quantise_rows(key, h)
+
+        def stage_one(g, extra):
+            for j in range(PACK):
+                for h in range(H):
+                    product(g, j, h)
+                    if g == 1:
+                        extra(j, h)
+                        if j + 1 < PACK:
+                            dw_pass(g, j + 1, h)
+                if g == 0 and j + 1 < PACK:
+                    quantise_g(j + 1, 0)
+                    quantise_g(j + 1, 1)
+                    for h in range(H):
+                        dw_pass(g, j + 1, h)
+                    if j + 2 < PACK:
+                        turn(("g", j + 2), (2, 3), "ss")
+                if j > 0:
+                    turn_back(g, j - 1)
+                head_sum(g, j)
+                extra(j, 4)
+            turn_back(g, 3)
+
+        def extra_first(j, place):
+            pass
+
+        stage_one(0, extra_first)
+        rows_operand("q", 0, "ss")
+        rows_operand("q", 1, "ss")
+        load_pair(K0, k_rows[:, 0], 1)
+
+        def stage_two(g, extra):
+            for h in range(H):
+                for j in range(PACK):
+                    weighted_sum(g, h, j)
+                extra(h, 0)
+                finish_ds(g, h, 0)
+                finish_ds(g, h, 1)
+                turn_ds(g, h, "ss" if g == 0 else ("ss","ss","ss","sv")[h], 0 if h == H - 1 else g)
+                quantise_ds_q(g, h)
+                for pair in range(2 if g == 1 or h < 2 else 0):
+                    store(*grad_k_passes(g, h, pair, 0 if h == H - 1 else g), "ss" if g == 0 else ("ssss","ssss","ssss","svsv")[h][2 * pair : 2 * pair + 2])
+                quantise_ds_t(g, h)
+                if g == 1:
+                    for pair in range(2):
+                        store(*grad_q_passes(h, pair, g), ("sssv","ssvv","svsv","svsv")[h][2 * pair : 2 * pair + 2])
+                extra(h, 1)
+
+        def extra_b0(h, place):
+            if place == 1:
+                if h < 2:
+                    rows_operand("q", h + 2, "ss")
+                    load_w(1, h + 2, 0, 4)
+                if h == 1:
+                    load_pair(K1, k_rows[:, 1], 1)
+                    turn(("v", 1), (4 + used[0] % 4, 4 + (used[0] + 1) % 4), "ss")
+                    used[0] = used[0] + 2
+                    quantise_v(1)
+                if h >= 2:
+                    rows_operand(K0, h - 2, "ss")
+            if place == 0 and h == 3:
+                for hh in range(H):
+                    dw_pass(1, 0, hh)
+
+        stage_two(0, extra_b0)
+
+        def extra_second(j, place):
+            pass
+
+        stage_one(1, extra_second)
+        for h in range(2, H):
+            for pair in range(2):
+                store(*grad_k_passes(0, h, pair, 1), "ss")
+        rows_operand(K1, 0, "ss")
+        rows_operand(K1, 1, "ss")
+
+        def extra_b1(h, place):
+            if place == 0 and h < 2:
+                rows_operand(K0, h + 2, "ss")
+                rows_operand(K1, h + 2, "ss")
+
+        stage_two(1, extra_b1)

@@ -33,6 +33,7 @@ def tile_multiheadattention_pa_v_kernel(tc, query, k, value, w, grad_out, out_0,
     with ExitStack() as ctx:
         sb = ctx.enter_context(tc.tile_pool(name="sb", bufs=1))
         ps = ctx.enter_context(tc.psum_pool(name="ps", bufs=1))
+        ctx.enter_context(tc.manual_schedule())
 
         def bank(i):
             return ps.tile([P, PASS], F32, name="bank%d" % i, tag="bank%d" % i)
@@ -94,31 +95,36 @@ def tile_multiheadattention_pa_v_kernel(tc, query, k, value, w, grad_out, out_0,
             nc.sync.dma_start(out=wt[g, h][:, j0:j1, :], in_=w_rows[:, h, j0:j1, PASS * g : PASS * (g + 1)])
 
         ident = sb.tile([P, P], F32, name="ident", align_bytes=64)
+        zeros = sb.tile([P, PASS], BF16, name="zeros", align_bytes=64)
         grouped = {}
+        xt = {}
 
-        def turn(key, banks, engines):
+        def turn(key, half, b):
             words = raw[key][:].bitcast(F32) if key[0] == "g" else raw[key][:].rearrange("p b d -> p (b d)").bitcast(F32)
-            grouped[key] = staged("grouped", 3)
-            out_words = grouped[key][:].bitcast(F32)
-            for half in range(2):
-                xt = bank(banks[half])
-                for i in range(4):
-                    b, u = 2 * half + i // 2, i % 2
-                    nc.tensor.transpose(xt[:, i * P : (i + 1) * P], words[:, 256 * b + u : 256 * (b + 1) : 2], ident[:])
-                src = xt[:].rearrange("x (b u r) -> x b r u", b=2, u=2)
-                if key[0] == "g":
-                    dst = out_words.rearrange("x (b r u) -> x b r u", b=4, u=2)[:, 2 * half : 2 * half + 2]
-                    copy(engines[half], dst, src)
-                else:
-                    dst = out_words.rearrange("x (r b u) -> x r b u", b=4, u=2)[:, :, 2 * half : 2 * half + 2]
-                    copy(engines[half], dst, xt[:].rearrange("x (b u r) -> x r b u", b=2, u=2))
+            xt[key, half] = bank(b)
+            for i in range(4):
+                blk, u = 2 * half + i // 2, i % 2
+                nc.tensor.transpose(
+                    xt[key, half][:, i * P : (i + 1) * P], words[:, 256 * blk + u : 256 * (blk + 1) : 2], ident[:]
+                )
 
-        def interleave(key, h, engines):
+        def save_turned(key, half, engine):
+            if half == 0:
+                grouped[key] = staged("grouped", 3)
+            out_words = grouped[key][:].bitcast(F32)
+            if key[0] == "g":
+                dst = out_words.rearrange("x (b r u) -> x b r u", b=4, u=2)[:, 2 * half : 2 * half + 2]
+                copy(engine, dst, xt[key, half][:].rearrange("x (b u r) -> x b r u", b=2, u=2))
+            else:
+                dst = out_words.rearrange("x (r b u) -> x r b u", b=4, u=2)[:, :, 2 * half : 2 * half + 2]
+                copy(engine, dst, xt[key, half][:].rearrange("x (b u r) -> x r b u", b=2, u=2))
+
+        def interleave(key, h, a, engine):
             src = raw[key, h // 2][:, :, DH * (h % 2) : DH * (h % 2 + 1)].rearrange("p t (a c i) -> p a c t i", a=2, i=4)
-            grouped[key, h] = staged("grouped", 3)
+            if a == 0:
+                grouped[key, h] = staged("grouped", 3)
             dst = grouped[key, h][:].rearrange("p (a c i t) -> p a c t i", a=2, i=4, t=PACK)
-            for a in range(2):
-                copy(engines[a], dst[:, a], src[:, a])
+            copy(engine, dst[:, a], src[:, a])
 
         def quantise_rows(key, h):
             quantise((key, h), grouped[key, h][:], E4M3, "q" if key == "q" else "k", H if key == "q" else HALVES * H)
@@ -129,19 +135,22 @@ def tile_multiheadattention_pa_v_kernel(tc, query, k, value, w, grad_out, out_0,
         def quantise_v(g):
             quantise(("v", g), grouped["v", g][:], E4M3, "v", HALVES)
 
+        def warm(b, count):
+            idle = bank(b)
+            for i in range(count):
+                nc.tensor.matmul(idle[:], lhsT=zeros[:, :P], rhs=zeros[:], start=True, stop=True)
+
         dw = {}
         prod = {}
         r = {}
         r_turned = {}
-
-        def work_bank(g, i):
-            return bank(4 * (1 - g) + i % 4)
+        sums = {}
 
         def r_bank(g, j):
             return bank(4 * g + j)
 
-        def dw_pass(g, j, h):
-            dw[j, h] = work_bank(g, h)
+        def dw_pass(g, j, h, b):
+            dw[j, h] = bank(b)
             mx_pass(dw[j, h], ("g", j, h // 2), h % 2, ("v", g), True, True)
 
         def product(g, j, h):
@@ -151,16 +160,19 @@ def tile_multiheadattention_pa_v_kernel(tc, query, k, value, w, grad_out, out_0,
                 out=prod[h][:, j, :], in0=dw[j, h][:], scalar=SCALE, in1=wt[g, h][:, j, :], op0=ALU.mult, op1=ALU.mult
             )
 
-        def head_sum(g, j):
-            acc = r_bank(g, j)
-            for b in range(4):
+        def head_sum(g, j, blocks=range(4)):
+            if blocks[0] == 0:
+                sums[j] = r_bank(g, j)
+            for b in blocks:
                 cols = slice(b * P, (b + 1) * P)
                 for h in range(H):
                     nc.tensor.matmul(
-                        acc[:, cols], lhsT=prod[h][:, j, cols], rhs=ident[:], start=h == 0, stop=h == H - 1, is_transpose=True
+                        sums[j][:, cols], lhsT=prod[h][:, j, cols], rhs=ident[:], start=h == 0, stop=h == H - 1, is_transpose=True
                     )
+
+        def save_sum(j):
             r_turned[j] = sb.tile([P, PASS], F32, name="r_turned", tag="r_turned", bufs=2, align_bytes=64)
-            nc.scalar.copy(out=r_turned[j][:], in_=acc[:])
+            nc.scalar.copy(out=r_turned[j][:], in_=sums[j][:])
 
         def turn_back(g, j):
             r[j] = r_bank(g, j)
@@ -170,11 +182,6 @@ def tile_multiheadattention_pa_v_kernel(tc, query, k, value, w, grad_out, out_0,
 
         ds_q = {}
         ds_t = {}
-        used = {0: 0, 1: 0}
-
-        def next_bank(g):
-            used[g] = used[g] + 1
-            return work_bank(g, used[g] - 1)
 
         def weighted_sum(g, h, j):
             nc.vector.tensor_tensor(out=wt[g, h][:, j, :], in0=r[j][:], in1=wt[g, h][:, j, :], op=ALU.mult)
@@ -190,164 +197,319 @@ def tile_multiheadattention_pa_v_kernel(tc, query, k, value, w, grad_out, out_0,
                 op=ALU.subtract,
             )
 
-        def turn_ds(g, h, engines, bank_half):
+        turned = {}
+
+        def turn_ds(h, u, banks):
             words = ds_q[h][:].bitcast(F32)
-            ds_t[h] = staged("ds_t", 2)
-            xt = [next_bank(bank_half), next_bank(bank_half)]
-            for u in range(2):
-                for jj in range(2):
-                    for s in (2 * u, 2 * u + 1):
-                        nc.tensor.transpose(
-                            xt[jj][:, s * P : (s + 1) * P], words[:, 256 * s + jj : 256 * (s + 1) : 2], ident[:]
-                        )
+            if u == 0:
+                turned[h] = [bank(banks[0]), bank(banks[1])]
             for jj in range(2):
-                copy(
-                    engines[jj],
-                    ds_t[h][:, 1024 * jj : 1024 * (jj + 1)].rearrange("m (e p s) -> m e p s", e=2, s=PACK),
-                    xt[jj][:].bitcast(BF16).rearrange("m (s p e) -> m e p s", s=PACK, e=2),
-                )
+                for s in (2 * u, 2 * u + 1):
+                    nc.tensor.transpose(
+                        turned[h][jj][:, s * P : (s + 1) * P], words[:, 256 * s + jj : 256 * (s + 1) : 2], ident[:]
+                    )
 
-        def store(accs, rows, h, engines):
-            result = io_tile([P, 2, DH], F32)
-            for i in range(2):
-                copy(engines[i], result[:, i, :], accs[i][:])
-            nc.sync.dma_start(out=rows[:, :, DH * h : DH * (h + 1)], in_=result[:])
+        def save_ds_t(h, jj, engine):
+            if jj == 0:
+                ds_t[h] = staged("ds_t", 2)
+            copy(
+                engine,
+                ds_t[h][:, 1024 * jj : 1024 * (jj + 1)].rearrange("m (e p s) -> m e p s", e=2, s=PACK),
+                turned[h][jj][:].bitcast(BF16).rearrange("m (s p e) -> m e p s", s=PACK, e=2),
+            )
 
-        def grad_k_passes(g, h, pair, bank_half):
-            accs = []
-            for s in (2 * pair, 2 * pair + 1):
-                accs.append(next_bank(bank_half))
-                mx_pass(accs[-1], ("ds_q", g, h), s, ("q", h), True, True)
-            return accs, dk_rows[:, g, 2 * pair : 2 * pair + 2], h
+        acc = {}
+        result = {}
 
-        def grad_q_passes(h, pair, bank_half):
-            accs = []
-            for j in (2 * pair, 2 * pair + 1):
-                accs.append(next_bank(bank_half))
-                for g in range(HALVES):
-                    mx_pass(accs[-1], ("ds_t", g, h, j // 2), j % 2, (("k", g), h), g == 0, g == HALVES - 1)
-            return accs, dq_rows[:, 2 * pair : 2 * pair + 2], h
+        def grad_k(g, h, s, b):
+            acc["k", g, h, s] = bank(b)
+            mx_pass(acc["k", g, h, s], ("ds_q", g, h), s, ("q", h), True, True)
+
+        def grad_q(h, j, b):
+            acc["q", 0, h, j] = bank(b)
+            for g in range(HALVES):
+                mx_pass(acc["q", 0, h, j], ("ds_t", g, h, j // 2), j % 2, (("k", g), h), g == 0, g == HALVES - 1)
+
+        def save(kind, g, h, i, engine, rows_per_store=2):
+            first = i - i % rows_per_store
+            if i == first:
+                if rows_per_store == 2:
+                    result[kind] = io_tile([P, 2, DH], F32)
+                elif kind == "k":
+                    result[kind] = sb.tile([P, 1, DH], F32, name="pair", tag="pair", bufs=4, align_bytes=64)
+                else:
+                    result[kind] = sb.tile([P, 1, DH], F32, name="wt", tag="wt", bufs=6, align_bytes=64)
+            copy(engine, result[kind][:, i - first, :], acc[kind, g, h, i][:])
+            if i == first + rows_per_store - 1:
+                rows = dk_rows[:, g] if kind == "k" else dq_rows
+                nc.sync.dma_start(out=rows[:, first : i + 1, DH * h : DH * (h + 1)], in_=result[kind][:])
 
         def quantise_ds_q(g, h):
             quantise(("ds_q", g, h), ds_q[h][:], E5M2, "ds_q", 4)
 
-        def quantise_ds_t(g, h):
-            for jj in range(2):
-                quantise(("ds_t", g, h, jj), ds_t[h][:, 1024 * jj : 1024 * (jj + 1)], E5M2, "ds_t", 2 * H + 4)
+        def quantise_ds_t(g, h, jj):
+            quantise(("ds_t", g, h, jj), ds_t[h][:, 1024 * jj : 1024 * (jj + 1)], E5M2, "ds_t", 2 * H + 4)
 
         K0, K1 = ("k", 0), ("k", 1)
         load_v(0)
         load_g(0)
-        load_w(0, 0, 0, 2)
         load_g(1)
+        load_w(0, 0, 0, 2)
         load_w(0, 1, 0, 2)
-        load_w(0, 2, 0, 2)
-        load_w(0, 3, 0, 2)
         load_g(2)
-        load_pair("q", q_rows, 0)
+        load_w(0, 2, 0, 2)
         load_g(3)
-        for h in range(H):
-            load_w(0, h, 2, 4)
+        load_w(0, 3, 0, 2)
+        load_w(0, 0, 2, 4)
+        load_pair("q", q_rows, 0)
+        load_w(0, 1, 2, 4)
+        load_w(0, 2, 2, 4)
+        load_w(0, 3, 2, 4)
         load_pair("q", q_rows, 1)
         load_pair(K0, k_rows[:, 0], 0)
         load_pair(K1, k_rows[:, 1], 0)
+        nc.vector.memset(zeros[:], 0.0)
         make_identity(nc, ident[:])
 
-        turn(("v", 0), (4, 5), "sv")
-        turn(("g", 0), (6, 7), "ss")
+        def tile_s(key, h):
+            interleave(key, h, 0, "s")
+            interleave(key, h, 1, "s")
+
+        def tile_e(key, h, engines):
+            interleave(key, h, 0, engines[0])
+            interleave(key, h, 1, engines[1])
+
+        def turn_g(j, banks):
+            for half in range(2):
+                turn(("g", j), half, banks[half])
+                save_turned(("g", j), half, "s")
+
+        warm(7, 6)
+        turn(("v", 0), 0, 4)
+        save_turned(("v", 0), 0, "s")
+        turn(("v", 0), 1, 5)
+        save_turned(("v", 0), 1, "v")
+        warm(3, 2)
+        turn_g(0, (6, 7))
         load_v(1)
         load_w(1, 0, 0, 4)
         load_w(1, 1, 0, 4)
+        turn_g(1, (0, 1))
         quantise_v(0)
         quantise_g(0, 0)
-        dw_pass(0, 0, 0)
-        dw_pass(0, 0, 1)
+        dw_pass(0, 0, 0, 4)
+        dw_pass(0, 0, 1, 5)
         quantise_g(0, 1)
-        dw_pass(0, 0, 2)
-        dw_pass(0, 0, 3)
-        turn(("g", 1), (0, 1), "ss")
-
-        def rows_operand(key, h, engines):
-            interleave(key, h, engines)
-            quantise_rows(key, h)
-
-        def stage_one(g, extra):
-            for j in range(PACK):
-                for h in range(H):
-                    product(g, j, h)
-                    if g == 1:
-                        extra(j, h)
-                        if j + 1 < PACK:
-                            dw_pass(g, j + 1, h)
-                if g == 0 and j + 1 < PACK:
-                    quantise_g(j + 1, 0)
-                    quantise_g(j + 1, 1)
-                    for h in range(H):
-                        dw_pass(g, j + 1, h)
-                    if j + 2 < PACK:
-                        turn(("g", j + 2), (2, 3), "ss")
-                if j > 0:
-                    turn_back(g, j - 1)
-                head_sum(g, j)
-                extra(j, 4)
-            turn_back(g, 3)
-
-        def extra_first(j, place):
-            pass
-
-        stage_one(0, extra_first)
-        rows_operand("q", 0, "ss")
-        rows_operand("q", 1, "ss")
+        product(0, 0, 0)
+        quantise_g(1, 0)
+        dw_pass(0, 1, 0, 2)
+        dw_pass(0, 1, 1, 3)
+        product(0, 0, 1)
+        quantise_g(1, 1)
+        turn_g(2, (0, 1))
+        dw_pass(0, 0, 2, 6)
+        dw_pass(0, 1, 2, 7)
+        product(0, 1, 0)
+        product(0, 1, 1)
+        dw_pass(0, 0, 3, 4)
+        dw_pass(0, 1, 3, 5)
+        quantise_g(2, 0)
+        quantise_g(2, 1)
+        turn_g(3, (0, 1))
+        product(0, 0, 2)
+        product(0, 1, 2)
+        dw_pass(0, 2, 0, 2)
+        dw_pass(0, 2, 1, 3)
+        product(0, 0, 3)
+        quantise_g(3, 0)
+        product(0, 1, 3)
+        quantise_g(3, 1)
+        head_sum(0, 0)
+        save_sum(0)
+        interleave("q", 0, 0, "s")
+        interleave("q", 0, 1, "s")
+        dw_pass(0, 3, 0, 6)
+        dw_pass(0, 3, 1, 7)
+        dw_pass(0, 2, 2, 4)
+        dw_pass(0, 3, 2, 5)
+        head_sum(0, 1)
+        turn_back(0, 0)
+        save_sum(1)
+        interleave("q", 1, 0, "s")
+        interleave("q", 1, 1, "s")
+        product(0, 2, 0)
+        product(0, 3, 0)
+        product(0, 2, 1)
+        dw_pass(0, 2, 3, 2)
+        dw_pass(0, 3, 3, 3)
+        turn_back(0, 1)
+        product(0, 3, 1)
+        product(0, 2, 2)
+        product(0, 3, 2)
+        weighted_sum(0, 0, 0)
+        product(0, 2, 3)
+        product(0, 3, 3)
+        warm(4, 2)
+        head_sum(0, 2)
+        save_sum(2)
+        warm(5, 2)
+        head_sum(0, 3)
         load_pair(K0, k_rows[:, 0], 1)
+        turn_back(0, 2)
+        save_sum(3)
+        turn_back(0, 3)
+        for h, j in ((0, 1), (1, 0), (1, 1)):
+            weighted_sum(0, h, j)
+        quantise_rows("q", 0)
+        tile_e("q", 2, "ss")
+        for h, j in ((2, 0), (2, 1), (0, 2), (1, 2)):
+            weighted_sum(0, h, j)
+        quantise_rows("q", 1)
+        tile_e("q", 3, "ss")
+        load_pair(K1, k_rows[:, 1], 1)
+        weighted_sum(0, 0, 3)
+        weighted_sum(0, 1, 3)
 
-        def stage_two(g, extra):
-            for h in range(H):
-                for j in range(PACK):
-                    weighted_sum(g, h, j)
-                extra(h, 0)
-                finish_ds(g, h, 0)
-                finish_ds(g, h, 1)
-                turn_ds(g, h, "ss" if g == 0 else ("ss","ss","ss","sv")[h], 0 if h == H - 1 else g)
-                quantise_ds_q(g, h)
-                for pair in range(2 if g == 1 or h < 2 else 0):
-                    store(*grad_k_passes(g, h, pair, 0 if h == H - 1 else g), "ss" if g == 0 else ("ssss","ssss","ssss","svsv")[h][2 * pair : 2 * pair + 2])
-                quantise_ds_t(g, h)
-                if g == 1:
-                    for pair in range(2):
-                        store(*grad_q_passes(h, pair, g), ("sssv","ssvv","svsv","svsv")[h][2 * pair : 2 * pair + 2])
-                extra(h, 1)
-
-        def extra_b0(h, place):
-            if place == 1:
-                if h < 2:
-                    rows_operand("q", h + 2, "ss")
-                    load_w(1, h + 2, 0, 4)
-                if h == 1:
-                    load_pair(K1, k_rows[:, 1], 1)
-                    turn(("v", 1), (4 + used[0] % 4, 4 + (used[0] + 1) % 4), "ss")
-                    used[0] = used[0] + 2
-                    quantise_v(1)
-                if h >= 2:
-                    rows_operand(K0, h - 2, "ss")
-            if place == 0 and h == 3:
+        for h in range(H):
+            b = 4 + 2 * (h % 2)
+            finish_ds(0, h, 0)
+            turn_ds(h, 0, (b, b + 1))
+            finish_ds(0, h, 1)
+            turn_ds(h, 1, (b, b + 1))
+            if h < 2:
+                load_w(1, h + 2, 0, 4)
+            if h == 0:
+                quantise_rows("q", 2)
+                tile_e(K0, 0, "ss")
+            if h == 1:
+                quantise_rows("q", 3)
+            if h > 0:
+                quantise_ds_t(0, h - 1, 0)
+                quantise_ds_t(0, h - 1, 1)
+            save_ds_t(h, 0, "s")
+            save_ds_t(h, 1, "s")
+            if h == 3:
+                break
+            todo = ((), (2, 3), (0, 1, 2, 3))[h]
+            for j in todo[:1]:
+                weighted_sum(0, h + 1, j)
+            quantise_ds_q(0, h)
+            for j in todo[1:]:
+                weighted_sum(0, h + 1, j)
+            if h == 1:
+                quantise_rows(K0, 0)
+                for half in range(2):
+                    turn(("v", 1), half, 4 + half)
+                    save_turned(("v", 1), half, "s")
+            if h < 2:
+                o = 10 - b
+                for s in range(PACK):
+                    grad_k(0, h, s, (o, o + 1, b, b + 1)[s])
+                    save("k", 0, h, s, "s")
+            if h == 2:
+                quantise_v(1)
                 for hh in range(H):
-                    dw_pass(1, 0, hh)
+                    dw_pass(1, 0, hh, hh)
+                tile_e(K1, 0, "ss")
 
-        stage_two(0, extra_b0)
+        late = [(h, s) for h in range(2, H) for s in range(PACK)]
+        tiles = ([(K0, 1, "ss")], [(K1, 1, "ss")], [(K0, 2, "ss")], [])
+        quants = ([(K1, 0)], [], [(K0, 1)], [(K1, 1)])
+        for j in range(PACK):
+            if j > 0:
+                head_sum(1, j - 1, range(2))
+            if j > 1:
+                turn_back(1, j - 2)
+            for h in range(H):
+                product(1, j, h)
+                if j + 1 < PACK:
+                    dw_pass(1, j + 1, h, h)
+                elif h < 3:
+                    grad_k(0, *late[h], h)
+                if j == 0 and h == 0:
+                    quantise_ds_q(0, 3)
+                if h == 1 and j > 0:
+                    head_sum(1, j - 1, range(2, 4))
+                    save_sum(j - 1)
+            if j == 1:
+                quantise_ds_t(0, 3, 0)
+                quantise_ds_t(0, 3, 1)
+            for key in quants[j]:
+                quantise_rows(*key)
+            for key in tiles[j]:
+                tile_e(*key)
+        save("k", 0, *late[0], "s")
+        save("k", 0, *late[1], "s")
+        head_sum(1, 3)
+        turn_back(1, 2)
+        save_sum(3)
+        grad_k(0, *late[3], 3)
+        turn_back(1, 3)
+        if len(late) > 4:
+            grad_k(0, *late[4], 0)
+        for i in range(2, len(late)):
+            save("k", 0, *late[i], "s")
+            if i + 3 < len(late):
+                grad_k(0, *late[i + 3], (i + 3) % 4)
+        for h, j in ((0, 0), (0, 1), (1, 0), (1, 1)):
+            weighted_sum(1, h, j)
+        quantise_rows(K0, 2)
+        for h, j in ((0, 2), (1, 2), (2, 0), (0, 3), (2, 1)):
+            weighted_sum(1, h, j)
+        tile_e(K1, 2, "ss")
 
-        def extra_second(j, place):
-            pass
-
-        stage_one(1, extra_second)
-        for h in range(2, H):
-            for pair in range(2):
-                store(*grad_k_passes(0, h, pair, 1), "ss")
-        rows_operand(K1, 0, "ss")
-        rows_operand(K1, 1, "ss")
-
-        def extra_b1(h, place):
-            if place == 0 and h < 2:
-                rows_operand(K0, h + 2, "ss")
-                rows_operand(K1, h + 2, "ss")
-
-        stage_two(1, extra_b1)
+        tiles = ([(K0, 3, "vv")], [(K1, 3, "vv")], [])
+        quants = ([(K1, 2)], [(K0, 3)], [(K1, 3)])
+        for h in range(H):
+            last = h == H - 1
+            b = 2 * (h % 2)
+            o = 2 - b
+            if last:
+                b = 4
+            finish_ds(1, h, 0)
+            turn_ds(h, 0, (b, b + 1))
+            finish_ds(1, h, 1)
+            turn_ds(h, 1, (b, b + 1))
+            if last:
+                break
+            save_ds_t(h, 0, "s")
+            save_ds_t(h, 1, "s")
+            todo = ((3,), (3,), (0, 1, 2, 3))[h]
+            weighted_sum(1, h + 1, todo[0])
+            quantise_ds_q(1, h)
+            grad_k(1, h, 0, o)
+            grad_k(1, h, 1, o + 1)
+            for j in todo[1:3]:
+                weighted_sum(1, h + 1, j)
+            for key in tiles[h]:
+                tile_e(*key)
+            if h == 0:
+                weighted_sum(1, 2, 2)
+            quantise_ds_t(1, h, 0)
+            save("k", 1, h, 0, "sss"[h])
+            grad_k(1, h, 2, b)
+            grad_k(1, h, 3, b + 1)
+            for j in todo[3:]:
+                weighted_sum(1, h + 1, j)
+            quantise_ds_t(1, h, 1)
+            for key in quants[h]:
+                quantise_rows(*key)
+            for s in range(1, PACK):
+                save("k", 1, h, s, "s")
+            for j in range(PACK):
+                grad_q(h, j, (o, o + 1, b, b + 1)[j])
+                save("q", 0, h, j, ("ssss","ssss","ssss")[h][j])
+        h = H - 1
+        quantise_ds_q(1, h)
+        save_ds_t(h, 0, "s")
+        save_ds_t(h, 1, "v")
+        for s, b in enumerate((6, 7, 2, 3)):
+            grad_k(1, h, s, b)
+        quantise_ds_t(1, h, 0)
+        quantise_ds_t(1, h, 1)
+        for j, b in enumerate((0, 1, 4, 5)):
+            grad_q(h, j, b)
+        for s in range(PACK):
+            save("k", 1, h, s, "ssvv"[s], 1)
+        for j in range(PACK):
+            save("q", 0, h, j, "svsv"[j], 1)

@@ -11,505 +11,521 @@ E4M3 = mybir.dt.float8_e4m3fn_x4
 E5M2 = mybir.dt.float8_e5m2_x4
 ALU = mybir.AluOpType
 
+TQ, TV, H, DH = 512, 1024, 4, 512
 P = 128
 PACK = 4
 PASS = P * PACK
-TQ, TV, H, DH = 512, 1024, 4, 512
 HALVES = TV // PASS
-SCALE = DH ** -0.5
+WORDS = PASS // 2
+BANKS = 8
+SCALE = DH**-0.5
 FLOPS = 3 * 2 * H * TQ * TV * DH
+
+STAGE_BUFS = 5
+PAIR_BUFS = 4
+W_BUFS = 6
+GROUPED_BUFS = 3
+DS_BUFS = 2
+LATE_HEADS = 2
 
 
 def tile_multiheadattention_pa_v_kernel(tc, query, k, value, w, grad_out, out_0, out_1):
     nc = tc.nc
+    scalar, vector, gpsimd = nc.scalar, nc.vector, nc.gpsimd
     q_rows = query.rearrange("b (p j) d -> p (b j) d", j=PACK)
     g_rows = grad_out.rearrange("b (p j) d -> p (b j) d", j=PACK)
-    k_rows = k.rearrange("b (g m s) d -> m (b g) s d", g=HALVES, s=PACK)
-    v_rows = value.rearrange("b (g m s) d -> m (b g) s d", g=HALVES, s=PACK)
     w_rows = w.rearrange("b h (p j) t -> p (b h) j t", j=PACK)
     dq_rows = out_0.rearrange("b (p j) d -> p (b j) d", j=PACK)
+    k_rows = k.rearrange("b (g m s) d -> m (b g) s d", g=HALVES, s=PACK)
+    v_rows = value.rearrange("b (g m s) d -> m (b g) s d", g=HALVES, s=PACK)
     dk_rows = out_1.rearrange("b (g m s) d -> m (b g) s d", g=HALVES, s=PACK)
+    Q, K0, K1 = "query", "k0", "k1"
+    row_operand = {Q: q_rows, K0: k_rows[:, 0], K1: k_rows[:, 1]}
 
     with ExitStack() as ctx:
         sb = ctx.enter_context(tc.tile_pool(name="sb", bufs=1))
         ps = ctx.enter_context(tc.psum_pool(name="ps", bufs=1))
         ctx.enter_context(tc.manual_schedule())
 
-        def bank(i):
-            return ps.tile([P, PASS], F32, name="bank%d" % i, tag="bank%d" % i)
+        def sbuf(tag, shape, dtype, bufs):
+            return sb.tile(shape, dtype, name=tag, tag=tag, bufs=bufs, align_bytes=64)
+
+        free_banks = list(range(BANKS))
+        held = {}
+
+        def take_bank(key, index=None):
+            if index is None:
+                index = free_banks.pop(0)
+            tile = ps.tile([P, PASS], F32, name="bank%d" % index, tag="bank%d" % index)
+            held[key] = (tile, index)
+            return tile
+
+        def give_bank(key):
+            free_banks.append(held.pop(key)[1])
 
         def copy(engine, out, in_):
-            if engine == "s":
+            if engine is scalar:
                 nc.scalar.copy(out=out, in_=in_)
             else:
                 nc.vector.tensor_copy(out=out, in_=in_)
-
-        def staged(tag, bufs):
-            return sb.tile([P, PACK * PASS], BF16, name=tag, tag=tag, bufs=bufs, align_bytes=64)
 
         mx = {}
 
         def quantise(key, values, fmt, tag, bufs):
             width = values.shape[1] // PACK
-            codes = sb.tile([P, width], U32, name=tag + "_codes", tag=tag + "_codes", bufs=bufs, align_bytes=64)
-            scales = sb.tile([P, width], U8, name=tag + "_scales", tag=tag + "_scales", bufs=bufs, align_bytes=64)
+            codes = sbuf(tag + "_codes", [P, width], U32, bufs)
+            scales = sbuf(tag + "_scales", [P, width], U8, bufs)
             nc.vector.quantize_mx(out=codes[:].bitcast(fmt), scales=scales[:], in_=values)
-            mx[key] = (codes, scales, fmt)
+            for block in range(width // P):
+                cols = slice(block * P, (block + 1) * P)
+                mx[key, block] = (codes[:, cols].bitcast(fmt), scales[:, cols])
+            mx[key] = (codes[:].bitcast(fmt), scales[:])
 
-        def mx_pass(acc, stationary, block, moving, start, stop):
-            s_codes, s_scales, s_fmt = mx[stationary]
-            m_codes, m_scales, m_fmt = mx[moving]
-            cols = slice(block * P, (block + 1) * P)
+        def mx_pass(acc, stationary, moving, start, stop):
             nc.tensor.matmul_mx(
                 out=acc[:],
-                lhsT=s_codes[:, cols].bitcast(s_fmt),
-                lhsT_scale=s_scales[:, cols],
-                rhs=m_codes[:].bitcast(m_fmt),
-                rhs_scale=m_scales[:],
+                lhsT=mx[stationary][0],
+                lhsT_scale=mx[stationary][1],
+                rhs=mx[moving][0],
+                rhs_scale=mx[moving][1],
                 start=start,
                 stop=stop,
             )
 
         raw = {}
-
-        def io_tile(shape, dtype):
-            return sb.tile(shape, dtype, name="io", tag="io", bufs=5, align_bytes=64)
-
-        def load_v(g):
-            raw["v", g] = io_tile([P, PACK, DH], BF16)
-            nc.sync.dma_start(out=raw["v", g][:], in_=v_rows[:, g])
-
-        def load_g(j):
-            raw["g", j] = io_tile([P, H * DH], BF16)
-            nc.sync.dma_start(out=raw["g", j][:], in_=g_rows[:, j])
-
-        def load_pair(key, rows, pair):
-            raw[key, pair] = sb.tile([P, PACK, 2 * DH], BF16, name="pair", tag="pair", bufs=4, align_bytes=64)
-            nc.sync.dma_start(out=raw[key, pair][:], in_=rows[:, :, 2 * DH * pair : 2 * DH * (pair + 1)])
-
         wt = {}
 
-        def load_w(g, h, j0, j1):
-            if j0 == 0:
-                wt[g, h] = sb.tile([P, PACK, PASS], F32, name="wt", tag="wt", bufs=6, align_bytes=64)
-            nc.sync.dma_start(out=wt[g, h][:, j0:j1, :], in_=w_rows[:, h, j0:j1, PASS * g : PASS * (g + 1)])
+        def load_v(g):
+            raw["v", g] = sbuf("stage", [P, PACK * DH], BF16, STAGE_BUFS)
+            nc.sync.dma_start(out=raw["v", g][:].rearrange("m (s d) -> m s d", s=PACK), in_=v_rows[:, g])
 
-        ident = sb.tile([P, P], F32, name="ident", align_bytes=64)
-        zeros = sb.tile([P, PASS], BF16, name="zeros", align_bytes=64)
+        def load_g(j):
+            raw["g", j] = sbuf("stage", [P, H * DH], BF16, STAGE_BUFS)
+            nc.sync.dma_start(out=raw["g", j][:], in_=g_rows[:, j])
+
+        def load_pair(key, pair):
+            raw[key, pair] = sbuf("pair", [P, PACK, 2 * DH], BF16, PAIR_BUFS)
+            nc.sync.dma_start(out=raw[key, pair][:], in_=row_operand[key][:, :, 2 * DH * pair : 2 * DH * (pair + 1)])
+
+        def load_w(g, h, rows):
+            if rows.start == 0:
+                wt[g, h] = sbuf("w", [P, PACK, PASS], F32, W_BUFS)
+            nc.sync.dma_start(out=wt[g, h][:, rows, :], in_=w_rows[:, h, rows, PASS * g : PASS * (g + 1)])
+
+        ident = sbuf("ident", [P, P], F32, 1)
+        zeros = sbuf("zeros", [P, PASS], BF16, 1)
         grouped = {}
-        xt = {}
 
-        def turn(key, half, b):
-            words = raw[key][:].bitcast(F32) if key[0] == "g" else raw[key][:].rearrange("p b d -> p (b d)").bitcast(F32)
-            xt[key, half] = bank(b)
-            for i in range(4):
-                blk, u = 2 * half + i // 2, i % 2
+        def turn(key, half, engine):
+            words = raw[key][:].bitcast(F32)
+            bank = take_bank("turn")
+            for i in range(PACK):
+                run, u = 2 * half + i // 2, i % 2
                 nc.tensor.transpose(
-                    xt[key, half][:, i * P : (i + 1) * P], words[:, 256 * blk + u : 256 * (blk + 1) : 2], ident[:]
+                    bank[:, i * P : (i + 1) * P], words[:, WORDS * run + u : WORDS * (run + 1) : 2], ident[:]
                 )
-
-        def save_turned(key, half, engine):
             if half == 0:
-                grouped[key] = staged("grouped", 3)
+                grouped[key] = sbuf("grouped", [P, PACK * PASS], BF16, GROUPED_BUFS)
             out_words = grouped[key][:].bitcast(F32)
+            runs = slice(2 * half, 2 * half + 2)
             if key[0] == "g":
-                dst = out_words.rearrange("x (b r u) -> x b r u", b=4, u=2)[:, 2 * half : 2 * half + 2]
-                copy(engine, dst, xt[key, half][:].rearrange("x (b u r) -> x b r u", b=2, u=2))
+                dst = out_words.rearrange("x (h p u) -> x h p u", h=H, u=2)[:, runs]
+                copy(engine, dst, bank[:].rearrange("x (h u p) -> x h p u", h=2, u=2))
             else:
-                dst = out_words.rearrange("x (r b u) -> x r b u", b=4, u=2)[:, :, 2 * half : 2 * half + 2]
-                copy(engine, dst, xt[key, half][:].rearrange("x (b u r) -> x r b u", b=2, u=2))
-
-        def interleave(key, h, a, engine):
-            src = raw[key, h // 2][:, :, DH * (h % 2) : DH * (h % 2 + 1)].rearrange("p t (a c i) -> p a c t i", a=2, i=4)
-            if a == 0:
-                grouped[key, h] = staged("grouped", 3)
-            dst = grouped[key, h][:].rearrange("p (a c i t) -> p a c t i", a=2, i=4, t=PACK)
-            copy(engine, dst[:, a], src[:, a])
-
-        def quantise_rows(key, h):
-            quantise((key, h), grouped[key, h][:], E4M3, "q" if key == "q" else "k", H if key == "q" else HALVES * H)
-
-        def quantise_g(j, pair):
-            quantise(("g", j, pair), grouped["g", j][:, 1024 * pair : 1024 * (pair + 1)], E5M2, "g", 2 * PACK)
+                dst = out_words.rearrange("x (m s u) -> x m s u", s=PACK, u=2)[:, :, runs]
+                copy(engine, dst, bank[:].rearrange("x (s u m) -> x m s u", s=2, u=2))
+            give_bank("turn")
 
         def quantise_v(g):
             quantise(("v", g), grouped["v", g][:], E4M3, "v", HALVES)
 
-        def warm(b, count):
-            idle = bank(b)
+        def quantise_g(j, pair):
+            quantise(("g", j, pair), grouped["g", j][:, 2 * PASS * pair : 2 * PASS * (pair + 1)], E5M2, "g", 2 * PACK)
+
+        def interleave(key, h, engines):
+            grouped[key, h] = sbuf("grouped", [P, PACK * DH], BF16, GROUPED_BUFS)
+            parts = 1 if engines[1] is gpsimd else 2
+            cols = DH // parts
+            for a in range(parts):
+                first = DH * (h % 2) + cols * a
+                src = raw[key, h // 2][:, :, first : first + cols]
+                dst = grouped[key, h][:, PACK * cols * a : PACK * cols * (a + 1)]
+                if engines[a] is gpsimd:
+                    nc.gpsimd.tensor_scalar(
+                        out=dst.rearrange("p (c j) -> p c j", j=PACK),
+                        in0=src.rearrange("p j c -> p c j"),
+                        scalar1=1.0,
+                        scalar2=0.0,
+                        op0=ALU.mult,
+                        op1=ALU.add,
+                    )
+                else:
+                    copy(
+                        engines[a],
+                        dst.rearrange("p (c i j) -> p c j i", i=4, j=PACK),
+                        src.rearrange("p j (c i) -> p c j i", i=4),
+                    )
+
+        def quantise_rows(key, h):
+            quantise((key, h), grouped[key, h][:], E4M3, key, H)
+
+        def warm(count):
+            bank = take_bank("warm")
             for i in range(count):
-                nc.tensor.matmul(idle[:], lhsT=zeros[:, :P], rhs=zeros[:], start=True, stop=True)
+                nc.tensor.matmul(bank[:], lhsT=zeros[:, :P], rhs=zeros[:], start=True, stop=True)
+            give_bank("warm")
 
-        dw = {}
         prod = {}
-        r = {}
         r_turned = {}
-        sums = {}
 
-        def r_bank(g, j):
-            return bank(4 * g + j)
+        def dw_pass(g, j, h):
+            mx_pass(take_bank(("dw", j, h)), (("g", j, h // 2), h % 2), ("v", g), True, True)
 
-        def dw_pass(g, j, h, b):
-            dw[j, h] = bank(b)
-            mx_pass(dw[j, h], ("g", j, h // 2), h % 2, ("v", g), True, True)
+        def dw_pair(g, j, pair):
+            dw_pass(g, j, 2 * pair)
+            dw_pass(g, j, 2 * pair + 1)
 
         def product(g, j, h):
             if j == 0:
-                prod[h] = sb.tile([P, PACK, PASS], F32, name="prod", tag="prod", bufs=H, align_bytes=64)
+                prod[h] = sbuf("prod", [P, PACK, PASS], F32, H)
             nc.vector.scalar_tensor_tensor(
-                out=prod[h][:, j, :], in0=dw[j, h][:], scalar=SCALE, in1=wt[g, h][:, j, :], op0=ALU.mult, op1=ALU.mult
+                out=prod[h][:, j, :],
+                in0=held["dw", j, h][0][:],
+                scalar=SCALE,
+                in1=wt[g, h][:, j, :],
+                op0=ALU.mult,
+                op1=ALU.mult,
             )
+            give_bank(("dw", j, h))
 
-        def head_sum(g, j, blocks=range(4)):
-            if blocks[0] == 0:
-                sums[j] = r_bank(g, j)
-            for b in blocks:
+        def head_sum(j, half):
+            bank = take_bank(("r", j)) if half == 0 else held["r", j][0]
+            for b in (2 * half, 2 * half + 1):
                 cols = slice(b * P, (b + 1) * P)
                 for h in range(H):
                     nc.tensor.matmul(
-                        sums[j][:, cols], lhsT=prod[h][:, j, cols], rhs=ident[:], start=h == 0, stop=h == H - 1, is_transpose=True
+                        bank[:, cols],
+                        lhsT=prod[h][:, j, cols],
+                        rhs=ident[:],
+                        start=h == 0,
+                        stop=h == H - 1,
+                        is_transpose=True,
                     )
 
         def save_sum(j):
-            r_turned[j] = sb.tile([P, PASS], F32, name="r_turned", tag="r_turned", bufs=2, align_bytes=64)
-            nc.scalar.copy(out=r_turned[j][:], in_=sums[j][:])
+            r_turned[j] = sbuf("r_turned", [P, PASS], F32, 2)
+            nc.scalar.copy(out=r_turned[j][:], in_=held["r", j][0][:])
 
-        def turn_back(g, j):
-            r[j] = r_bank(g, j)
-            for b in range(4):
+        def turn_back(j):
+            bank = take_bank(("r", j), held["r", j][1])
+            for b in range(PACK):
                 cols = slice(b * P, (b + 1) * P)
-                nc.tensor.transpose(r[j][:, cols], r_turned[j][:, cols], ident[:])
+                nc.tensor.transpose(bank[:, cols], r_turned[j][:, cols], ident[:])
 
         ds_q = {}
         ds_t = {}
+        r_readers = {}
 
-        def weighted_sum(g, h, j):
-            nc.vector.tensor_tensor(out=wt[g, h][:, j, :], in0=r[j][:], in1=wt[g, h][:, j, :], op=ALU.mult)
+        def times_r(g, h, j):
+            nc.vector.tensor_tensor(out=wt[g, h][:, j, :], in0=held["r", j][0][:], in1=wt[g, h][:, j, :], op=ALU.mult)
+            r_readers[g, j] = r_readers.get((g, j), 0) + 1
+            if r_readers[g, j] == H:
+                give_bank(("r", j))
 
-        def finish_ds(g, h, u):
-            if u == 0:
-                ds_q[h] = staged("ds_q", 2)
-            view = "p j (m u e) -> p u m j e"
-            nc.vector.tensor_tensor(
-                out=ds_q[h][:].rearrange("p (u e m j) -> p u m j e", u=2, e=2, j=PACK)[:, u],
-                in0=prod[h][:].rearrange(view, u=2, e=2)[:, u],
-                in1=wt[g, h][:].rearrange(view, u=2, e=2)[:, u],
-                op=ALU.subtract,
-            )
-
-        turned = {}
-
-        def turn_ds(h, u, banks):
+        def make_ds(g, h):
+            ds_q[h] = sbuf("ds_q", [P, PACK * PASS], BF16, DS_BUFS)
             words = ds_q[h][:].bitcast(F32)
-            if u == 0:
-                turned[h] = [bank(banks[0]), bank(banks[1])]
-            for jj in range(2):
-                for s in (2 * u, 2 * u + 1):
-                    nc.tensor.transpose(
-                        turned[h][jj][:, s * P : (s + 1) * P], words[:, 256 * s + jj : 256 * (s + 1) : 2], ident[:]
-                    )
+            banks = [take_bank(("ds", h, jj)) for jj in range(2)]
+            view = "p j (m u e) -> p u m j e"
+            for u in range(2):
+                nc.vector.tensor_tensor(
+                    out=ds_q[h][:].rearrange("p (u e m j) -> p u m j e", u=2, e=2, j=PACK)[:, u],
+                    in0=prod[h][:].rearrange(view, u=2, e=2)[:, u],
+                    in1=wt[g, h][:].rearrange(view, u=2, e=2)[:, u],
+                    op=ALU.subtract,
+                )
+                for jj in range(2):
+                    for s in (2 * u, 2 * u + 1):
+                        nc.tensor.transpose(
+                            banks[jj][:, s * P : (s + 1) * P], words[:, WORDS * s + jj : WORDS * (s + 1) : 2], ident[:]
+                        )
 
-        def save_ds_t(h, jj, engine):
-            if jj == 0:
-                ds_t[h] = staged("ds_t", 2)
+        def save_ds_t(h, rows, engine):
+            if rows.start == 0:
+                ds_t[h] = sbuf("ds_t", [P, PACK * PASS], BF16, DS_BUFS)
+            jj = rows.start // 2
+            src = held["ds", h, jj][0][:].bitcast(BF16).rearrange("m (s p e) -> m e p s", s=PACK, e=2)
             copy(
                 engine,
-                ds_t[h][:, 1024 * jj : 1024 * (jj + 1)].rearrange("m (e p s) -> m e p s", e=2, s=PACK),
-                turned[h][jj][:].bitcast(BF16).rearrange("m (s p e) -> m e p s", s=PACK, e=2),
+                ds_t[h][:].rearrange("m (j p s) -> m j p s", j=PACK, s=PACK)[:, rows],
+                src[:, rows.start - 2 * jj : rows.stop - 2 * jj],
             )
+            if rows.stop == 2 * jj + 2:
+                give_bank(("ds", h, jj))
 
-        acc = {}
-        result = {}
+        def quantise_ds(tiles, name, g, h, rows, bufs):
+            count = rows.stop - rows.start
+            key = (name, g, h, rows.start)
+            quantise(key, tiles[h][:, PASS * rows.start : PASS * rows.stop], E5M2, "%s%d" % (name, count), bufs)
+            for block in range(count):
+                mx[name, g, h, "block", rows.start + block] = mx[key, block]
 
-        def grad_k(g, h, s, b):
-            acc["k", g, h, s] = bank(b)
-            mx_pass(acc["k", g, h, s], ("ds_q", g, h), s, ("q", h), True, True)
-
-        def grad_q(h, j, b):
-            acc["q", 0, h, j] = bank(b)
-            for g in range(HALVES):
-                mx_pass(acc["q", 0, h, j], ("ds_t", g, h, j // 2), j % 2, (("k", g), h), g == 0, g == HALVES - 1)
-
-        def save(kind, g, h, i, engine, rows_per_store=2):
-            first = i - i % rows_per_store
-            if i == first:
-                if rows_per_store == 2:
-                    result[kind] = io_tile([P, 2, DH], F32)
-                elif kind == "k":
-                    result[kind] = sb.tile([P, 1, DH], F32, name="pair", tag="pair", bufs=4, align_bytes=64)
-                else:
-                    result[kind] = sb.tile([P, 1, DH], F32, name="wt", tag="wt", bufs=6, align_bytes=64)
-            copy(engine, result[kind][:, i - first, :], acc[kind, g, h, i][:])
-            if i == first + rows_per_store - 1:
-                rows = dk_rows[:, g] if kind == "k" else dq_rows
-                nc.sync.dma_start(out=rows[:, first : i + 1, DH * h : DH * (h + 1)], in_=result[kind][:])
+        ALL, LOW, HIGH = slice(0, 4), slice(0, 2), slice(2, 4)
 
         def quantise_ds_q(g, h):
-            quantise(("ds_q", g, h), ds_q[h][:], E5M2, "ds_q", 4)
+            quantise_ds(ds_q, "ds_q", g, h, ALL, LATE_HEADS + 1)
 
-        def quantise_ds_t(g, h, jj):
-            quantise(("ds_t", g, h, jj), ds_t[h][:, 1024 * jj : 1024 * (jj + 1)], E5M2, "ds_t", 2 * H + 4)
+        def grad_k(g, h, s):
+            mx_pass(take_bank(("dk", g, h, s)), ("ds_q", g, h, "block", s), (Q, h), True, True)
 
-        K0, K1 = ("k", 0), ("k", 1)
+        def grad_q(h, j):
+            bank = take_bank(("dq", h, j))
+            for g, key in enumerate((K0, K1)):
+                mx_pass(bank, ("ds_t", g, h, "block", j), (key, h), g == 0, g == HALVES - 1)
+
+        result = {}
+
+        def save(key, rows, engine):
+            h, i = key[-2:]
+            if i % 2 == 0:
+                result[key[0]] = sbuf("stage", [P, 2, DH], F32, STAGE_BUFS)
+            copy(engine, result[key[0]][:, i % 2, :], held[key][0][:])
+            give_bank(key)
+            if i % 2 == 1:
+                nc.sync.dma_start(out=rows[:, i - 1 : i + 1, DH * h : DH * (h + 1)], in_=result[key[0]][:])
+
+        def save_alone(key, rows, engine, tag, bufs):
+            h, i = key[-2:]
+            tile = sbuf(tag, [P, 1, DH], F32, bufs)
+            copy(engine, tile[:, 0, :], held[key][0][:])
+            give_bank(key)
+            nc.sync.dma_start(out=rows[:, i : i + 1, DH * h : DH * (h + 1)], in_=tile[:])
+
+        def save_k(g, h, s):
+            save(("dk", g, h, s), dk_rows[:, g], scalar)
+
+        on_scalar = (scalar, scalar)
+        on_gpsimd = (gpsimd, gpsimd)
+
         load_v(0)
         load_g(0)
         load_g(1)
-        load_w(0, 0, 0, 2)
-        load_w(0, 1, 0, 2)
+        load_w(0, 0, LOW)
+        load_w(0, 1, LOW)
         load_g(2)
-        load_w(0, 2, 0, 2)
+        load_w(0, 2, LOW)
         load_g(3)
-        load_w(0, 3, 0, 2)
-        load_w(0, 0, 2, 4)
-        load_pair("q", q_rows, 0)
-        load_w(0, 1, 2, 4)
-        load_w(0, 2, 2, 4)
-        load_w(0, 3, 2, 4)
-        load_pair("q", q_rows, 1)
-        load_pair(K0, k_rows[:, 0], 0)
-        load_pair(K1, k_rows[:, 1], 0)
+        load_w(0, 3, LOW)
+        load_w(0, 0, HIGH)
+        load_pair(Q, 0)
+        for h in range(1, H):
+            load_w(0, h, HIGH)
+        load_pair(Q, 1)
+        load_pair(K0, 0)
+        load_pair(K1, 0)
         nc.vector.memset(zeros[:], 0.0)
         make_identity(nc, ident[:])
 
-        def tile_s(key, h):
-            interleave(key, h, 0, "s")
-            interleave(key, h, 1, "s")
-
-        def tile_e(key, h, engines):
-            interleave(key, h, 0, engines[0])
-            interleave(key, h, 1, engines[1])
-
-        def turn_g(j, banks):
-            for half in range(2):
-                turn(("g", j), half, banks[half])
-                save_turned(("g", j), half, "s")
-
-        warm(7, 6)
-        turn(("v", 0), 0, 4)
-        save_turned(("v", 0), 0, "s")
-        turn(("v", 0), 1, 5)
-        save_turned(("v", 0), 1, "v")
-        warm(3, 2)
-        turn_g(0, (6, 7))
+        warm(6)
+        turn(("v", 0), 0, scalar)
+        turn(("v", 0), 1, vector)
+        warm(3)
+        turn(("g", 0), 0, scalar)
+        turn(("g", 0), 1, scalar)
         load_v(1)
-        load_w(1, 0, 0, 4)
-        load_w(1, 1, 0, 4)
-        turn_g(1, (0, 1))
+        load_w(1, 0, ALL)
+        load_w(1, 1, ALL)
+        warm(3)
         quantise_v(0)
         quantise_g(0, 0)
-        dw_pass(0, 0, 0, 4)
-        dw_pass(0, 0, 1, 5)
+        turn(("g", 1), 0, scalar)
+        dw_pair(0, 0, 0)
+        turn(("g", 1), 1, scalar)
         quantise_g(0, 1)
         product(0, 0, 0)
         quantise_g(1, 0)
-        dw_pass(0, 1, 0, 2)
-        dw_pass(0, 1, 1, 3)
+        turn(("g", 2), 0, scalar)
+        dw_pair(0, 0, 1)
         product(0, 0, 1)
         quantise_g(1, 1)
-        turn_g(2, (0, 1))
-        dw_pass(0, 0, 2, 6)
-        dw_pass(0, 1, 2, 7)
-        product(0, 1, 0)
-        product(0, 1, 1)
-        dw_pass(0, 0, 3, 4)
-        dw_pass(0, 1, 3, 5)
-        quantise_g(2, 0)
-        quantise_g(2, 1)
-        turn_g(3, (0, 1))
+        turn(("g", 2), 1, scalar)
+        dw_pair(0, 1, 0)
         product(0, 0, 2)
-        product(0, 1, 2)
-        dw_pass(0, 2, 0, 2)
-        dw_pass(0, 2, 1, 3)
+        quantise_g(2, 0)
+        turn(("g", 3), 0, scalar)
+        turn(("g", 3), 1, scalar)
+        dw_pair(0, 1, 1)
+        product(0, 1, 0)
+        quantise_g(2, 1)
         product(0, 0, 3)
+        product(0, 1, 1)
+        head_sum(0, 0)
+        head_sum(0, 1)
+        save_sum(0)
+        interleave(Q, 0, on_scalar)
+        dw_pair(0, 2, 0)
+        product(0, 1, 2)
         quantise_g(3, 0)
         product(0, 1, 3)
         quantise_g(3, 1)
-        head_sum(0, 0)
-        save_sum(0)
-        interleave("q", 0, 0, "s")
-        interleave("q", 0, 1, "s")
-        dw_pass(0, 3, 0, 6)
-        dw_pass(0, 3, 1, 7)
-        dw_pass(0, 2, 2, 4)
-        dw_pass(0, 3, 2, 5)
-        head_sum(0, 1)
-        turn_back(0, 0)
+        head_sum(1, 0)
+        dw_pair(0, 2, 1)
+        head_sum(1, 1)
         save_sum(1)
-        interleave("q", 1, 0, "s")
-        interleave("q", 1, 1, "s")
+        interleave(Q, 1, on_scalar)
         product(0, 2, 0)
-        product(0, 3, 0)
         product(0, 2, 1)
-        dw_pass(0, 2, 3, 2)
-        dw_pass(0, 3, 3, 3)
-        turn_back(0, 1)
-        product(0, 3, 1)
+        dw_pair(0, 3, 0)
+        turn_back(0)
         product(0, 2, 2)
-        product(0, 3, 2)
-        weighted_sum(0, 0, 0)
+        turn_back(1)
+        product(0, 3, 0)
+        dw_pair(0, 3, 1)
         product(0, 2, 3)
+        product(0, 3, 1)
+        times_r(0, 0, 0)
+        product(0, 3, 2)
         product(0, 3, 3)
-        warm(4, 2)
-        head_sum(0, 2)
+        head_sum(2, 0)
+        warm(2)
+        head_sum(2, 1)
         save_sum(2)
-        warm(5, 2)
-        head_sum(0, 3)
-        load_pair(K0, k_rows[:, 0], 1)
-        turn_back(0, 2)
+        head_sum(3, 0)
+        head_sum(3, 1)
+        load_pair(K0, 1)
+        turn_back(2)
         save_sum(3)
-        turn_back(0, 3)
+        turn_back(3)
         for h, j in ((0, 1), (1, 0), (1, 1)):
-            weighted_sum(0, h, j)
-        quantise_rows("q", 0)
-        tile_e("q", 2, "ss")
+            times_r(0, h, j)
+        quantise_rows(Q, 0)
+        interleave(Q, 2, on_scalar)
         for h, j in ((2, 0), (2, 1), (0, 2), (1, 2)):
-            weighted_sum(0, h, j)
-        quantise_rows("q", 1)
-        tile_e("q", 3, "ss")
-        load_pair(K1, k_rows[:, 1], 1)
-        weighted_sum(0, 0, 3)
-        weighted_sum(0, 1, 3)
+            times_r(0, h, j)
+        quantise_rows(Q, 1)
+        interleave(Q, 3, on_scalar)
+        load_pair(K1, 1)
+        times_r(0, 0, 3)
+        times_r(0, 1, 3)
 
-        for h in range(H):
-            b = 4 + 2 * (h % 2)
-            finish_ds(0, h, 0)
-            turn_ds(h, 0, (b, b + 1))
-            finish_ds(0, h, 1)
-            turn_ds(h, 1, (b, b + 1))
-            if h < 2:
-                load_w(1, h + 2, 0, 4)
+        def first_ds(h):
+            make_ds(0, h)
+            if h + 2 < H:
+                load_w(1, h + 2, ALL)
+                quantise_rows(Q, h + 2)
             if h == 0:
-                quantise_rows("q", 2)
-                tile_e(K0, 0, "ss")
-            if h == 1:
-                quantise_rows("q", 3)
-            if h > 0:
-                quantise_ds_t(0, h - 1, 0)
-                quantise_ds_t(0, h - 1, 1)
-            save_ds_t(h, 0, "s")
-            save_ds_t(h, 1, "s")
-            if h == 3:
-                break
-            todo = ((), (2, 3), (0, 1, 2, 3))[h]
-            for j in todo[:1]:
-                weighted_sum(0, h + 1, j)
-            quantise_ds_q(0, h)
-            for j in todo[1:]:
-                weighted_sum(0, h + 1, j)
-            if h == 1:
-                quantise_rows(K0, 0)
-                for half in range(2):
-                    turn(("v", 1), half, 4 + half)
-                    save_turned(("v", 1), half, "s")
-            if h < 2:
-                o = 10 - b
-                for s in range(PACK):
-                    grad_k(0, h, s, (o, o + 1, b, b + 1)[s])
-                    save("k", 0, h, s, "s")
-            if h == 2:
-                quantise_v(1)
-                for hh in range(H):
-                    dw_pass(1, 0, hh, hh)
-                tile_e(K1, 0, "ss")
+                interleave(K0, 0, on_scalar)
+            else:
+                quantise_ds(ds_t, "ds_t", 0, h - 1, ALL, H)
+            save_ds_t(h, LOW, scalar)
+            save_ds_t(h, HIGH, scalar)
 
-        late = [(h, s) for h in range(2, H) for s in range(PACK)]
-        tiles = ([(K0, 1, "ss")], [(K1, 1, "ss")], [(K0, 2, "ss")], [])
-        quants = ([(K1, 0)], [], [(K0, 1)], [(K1, 1)])
+        def grad_k_head(g, h):
+            for s in range(PACK):
+                grad_k(g, h, s)
+                save_k(g, h, s)
+
+        first_ds(0)
+        quantise_ds_q(0, 0)
+        grad_k_head(0, 0)
+        first_ds(1)
+        times_r(0, 2, 2)
+        quantise_ds_q(0, 1)
+        times_r(0, 2, 3)
+        quantise_rows(K0, 0)
+        turn(("v", 1), 0, scalar)
+        turn(("v", 1), 1, scalar)
+        grad_k_head(0, 1)
+        first_ds(2)
+        times_r(0, 3, 0)
+        quantise_ds_q(0, 2)
+        for j in range(1, PACK):
+            times_r(0, 3, j)
+        quantise_v(1)
+        for h in range(H):
+            dw_pass(1, 0, h)
+        interleave(K1, 0, on_scalar)
+        first_ds(3)
+
+        late = [(h, s) for h in range(H - LATE_HEADS, H) for s in range(PACK)]
         for j in range(PACK):
             if j > 0:
-                head_sum(1, j - 1, range(2))
+                head_sum(j - 1, 0)
             if j > 1:
-                turn_back(1, j - 2)
+                turn_back(j - 2)
             for h in range(H):
                 product(1, j, h)
                 if j + 1 < PACK:
-                    dw_pass(1, j + 1, h, h)
-                elif h < 3:
-                    grad_k(0, *late[h], h)
+                    dw_pass(1, j + 1, h)
+                elif h + 1 < H:
+                    grad_k(0, *late[h])
                 if j == 0 and h == 0:
-                    quantise_ds_q(0, 3)
-                if h == 1 and j > 0:
-                    head_sum(1, j - 1, range(2, 4))
+                    quantise_ds_q(0, H - 1)
+                if j > 0 and h == 1:
+                    head_sum(j - 1, 1)
                     save_sum(j - 1)
+            if j == 0:
+                quantise_rows(K1, 0)
+                interleave(K0, 1, on_scalar)
             if j == 1:
-                quantise_ds_t(0, 3, 0)
-                quantise_ds_t(0, 3, 1)
-            for key in quants[j]:
-                quantise_rows(*key)
-            for key in tiles[j]:
-                tile_e(*key)
-        save("k", 0, *late[0], "s")
-        save("k", 0, *late[1], "s")
-        head_sum(1, 3)
-        turn_back(1, 2)
+                quantise_ds(ds_t, "ds_t", 0, H - 1, ALL, H)
+                interleave(K1, 1, on_scalar)
+            if j == 2:
+                quantise_rows(K0, 1)
+                interleave(K0, 2, on_scalar)
+                interleave(K1, 2, on_gpsimd)
+        save_k(0, *late[0])
+        save_k(0, *late[1])
+        head_sum(3, 0)
+        head_sum(3, 1)
+        turn_back(2)
         save_sum(3)
-        grad_k(0, *late[3], 3)
-        turn_back(1, 3)
-        if len(late) > 4:
-            grad_k(0, *late[4], 0)
+        grad_k(0, *late[3])
+        turn_back(3)
+        grad_k(0, *late[4])
         for i in range(2, len(late)):
-            save("k", 0, *late[i], "s")
+            save_k(0, *late[i])
             if i + 3 < len(late):
-                grad_k(0, *late[i + 3], (i + 3) % 4)
-        for h, j in ((0, 0), (0, 1), (1, 0), (1, 1)):
-            weighted_sum(1, h, j)
+                grad_k(0, *late[i + 3])
+        times_r(1, 0, 0)
+        times_r(1, 0, 1)
         quantise_rows(K0, 2)
-        for h, j in ((0, 2), (1, 2), (2, 0), (0, 3), (2, 1)):
-            weighted_sum(1, h, j)
-        tile_e(K1, 2, "ss")
+        quantise_rows(K1, 1)
+        interleave(K0, 3, on_gpsimd)
+        interleave(K1, 3, (gpsimd, scalar))
+        for h, j in ((1, 0), (1, 1), (0, 2), (1, 2), (2, 0), (0, 3)):
+            times_r(1, h, j)
 
-        tiles = ([(K0, 3, "vv")], [(K1, 3, "vv")], [])
-        quants = ([(K1, 2)], [(K0, 3)], [(K1, 3)])
-        for h in range(H):
-            last = h == H - 1
-            b = 2 * (h % 2)
-            o = 2 - b
-            if last:
-                b = 4
-            finish_ds(1, h, 0)
-            turn_ds(h, 0, (b, b + 1))
-            finish_ds(1, h, 1)
-            turn_ds(h, 1, (b, b + 1))
-            if last:
-                break
-            save_ds_t(h, 0, "s")
-            save_ds_t(h, 1, "s")
-            todo = ((3,), (3,), (0, 1, 2, 3))[h]
-            weighted_sum(1, h + 1, todo[0])
+        left = (((1, 3), (2, 1), (3, 0), (3, 1)), ((2, 2), (2, 3)), ((3, 2), (3, 3)))
+        k_left = ((K1, 2), (K0, 3), (K1, 3))
+        for h in range(H - 1):
+            make_ds(1, h)
+            save_ds_t(h, LOW, scalar)
+            times_r(1, *left[h][0])
             quantise_ds_q(1, h)
-            grad_k(1, h, 0, o)
-            grad_k(1, h, 1, o + 1)
-            for j in todo[1:3]:
-                weighted_sum(1, h + 1, j)
-            for key in tiles[h]:
-                tile_e(*key)
-            if h == 0:
-                weighted_sum(1, 2, 2)
-            quantise_ds_t(1, h, 0)
-            save("k", 1, h, 0, "sss"[h])
-            grad_k(1, h, 2, b)
-            grad_k(1, h, 3, b + 1)
-            for j in todo[3:]:
-                weighted_sum(1, h + 1, j)
-            quantise_ds_t(1, h, 1)
-            for key in quants[h]:
-                quantise_rows(*key)
-            for s in range(1, PACK):
-                save("k", 1, h, s, "s")
+            save_ds_t(h, HIGH, vector if h == H - 2 else scalar)
+            grad_k_head(1, h)
+            for pair in left[h][1:]:
+                times_r(1, *pair)
+            quantise_rows(*k_left[h])
+            quantise_ds(ds_t, "ds_t", 1, h, LOW, PACK)
+            quantise_ds(ds_t, "ds_t", 1, h, HIGH, PACK)
             for j in range(PACK):
-                grad_q(h, j, (o, o + 1, b, b + 1)[j])
-                save("q", 0, h, j, ("ssss","ssss","ssss")[h][j])
+                grad_q(h, j)
+                save(("dq", h, j), dq_rows, scalar)
+
         h = H - 1
-        quantise_ds_q(1, h)
-        save_ds_t(h, 0, "s")
-        save_ds_t(h, 1, "v")
-        for s, b in enumerate((6, 7, 2, 3)):
-            grad_k(1, h, s, b)
-        quantise_ds_t(1, h, 0)
-        quantise_ds_t(1, h, 1)
-        for j, b in enumerate((0, 1, 4, 5)):
-            grad_q(h, j, b)
+        make_ds(1, h)
+        quantise_ds(ds_q, "ds_q", 1, h, LOW, 2)
+        quantise_ds(ds_q, "ds_q", 1, h, HIGH, 2)
         for s in range(PACK):
-            save("k", 1, h, s, "ssvv"[s], 1)
+            grad_k(1, h, s)
+            save_alone(("dk", 1, h, s), dk_rows[:, 1], scalar, "pair", PAIR_BUFS)
+        save_ds_t(h, slice(0, 1), vector)
         for j in range(PACK):
-            save("q", 0, h, j, "svsv"[j], 1)
+            if j + 1 < PACK:
+                save_ds_t(h, slice(j + 1, j + 2), vector)
+            quantise_ds(ds_t, "ds_t", 1, h, slice(j, j + 1), PACK)
+            grad_q(h, j)
+        for j in range(PACK):
+            save_alone(("dq", h, j), dq_rows, vector if j == PACK - 1 else scalar, "w", W_BUFS)

from contextlib import ExitStack

import concourse.mybir as mybir
from concourse.masks import make_identity

F32 = mybir.dt.float32
BF16 = mybir.dt.bfloat16
U32 = mybir.dt.uint32
U8 = mybir.dt.uint8
E4M3 = mybir.dt.float8_e4m3fn_x4
E5M2 = mybir.dt.float8_e5m2_x4
ALU = mybir.AluOpType

TQ, TV, H, DH = 512, 1024, 4, 512
P = 128
PACK = 4
PASS = P * PACK
HALVES = TV // PASS
WORDS = PASS // 2
BANKS = 8
SCALE = DH**-0.5
FLOPS = 3 * 2 * H * TQ * TV * DH

STAGE_BUFS = 5
PAIR_BUFS = 4
W_BUFS = 6
GROUPED_BUFS = 3
DS_BUFS = 2
LATE_HEADS = 2


def tile_multiheadattention_pa_v_kernel(tc, query, k, value, w, grad_out, out_0, out_1):
    nc = tc.nc
    scalar, vector, gpsimd = nc.scalar, nc.vector, nc.gpsimd
    q_rows = query.rearrange("b (p j) d -> p (b j) d", j=PACK)
    g_rows = grad_out.rearrange("b (p j) d -> p (b j) d", j=PACK)
    w_rows = w.rearrange("b h (p j) t -> p (b h) j t", j=PACK)
    dq_rows = out_0.rearrange("b (p j) d -> p (b j) d", j=PACK)
    k_rows = k.rearrange("b (g m s) d -> m (b g) s d", g=HALVES, s=PACK)
    v_rows = value.rearrange("b (g m s) d -> m (b g) s d", g=HALVES, s=PACK)
    dk_rows = out_1.rearrange("b (g m s) d -> m (b g) s d", g=HALVES, s=PACK)
    Q, K0, K1 = "query", "k0", "k1"
    row_operand = {Q: q_rows, K0: k_rows[:, 0], K1: k_rows[:, 1]}

    with ExitStack() as ctx:
        sb = ctx.enter_context(tc.tile_pool(name="sb", bufs=1))
        ps = ctx.enter_context(tc.psum_pool(name="ps", bufs=1))
        ctx.enter_context(tc.manual_schedule())

        def sbuf(tag, shape, dtype, bufs):
            return sb.tile(shape, dtype, name=tag, tag=tag, bufs=bufs, align_bytes=64)

        free_banks = list(range(BANKS))
        held = {}

        def take_bank(key, index=None):
            if index is None:
                index = free_banks.pop(0)
            tile = ps.tile([P, PASS], F32, name="bank%d" % index, tag="bank%d" % index)
            held[key] = (tile, index)
            return tile

        def give_bank(key):
            free_banks.append(held.pop(key)[1])

        def copy(engine, out, in_):
            if engine is scalar:
                nc.scalar.copy(out=out, in_=in_)
            else:
                nc.vector.tensor_copy(out=out, in_=in_)

        mx = {}

        def quantise(key, values, fmt, tag, bufs):
            width = values.shape[1] // PACK
            codes = sbuf(tag + "_codes", [P, width], U32, bufs)
            scales = sbuf(tag + "_scales", [P, width], U8, bufs)
            nc.vector.quantize_mx(out=codes[:].bitcast(fmt), scales=scales[:], in_=values)
            for block in range(width // P):
                cols = slice(block * P, (block + 1) * P)
                mx[key, block] = (codes[:, cols].bitcast(fmt), scales[:, cols])
            mx[key] = (codes[:].bitcast(fmt), scales[:])

        def mx_pass(acc, stationary, moving, start, stop):
            nc.tensor.matmul_mx(
                out=acc[:],
                lhsT=mx[stationary][0],
                lhsT_scale=mx[stationary][1],
                rhs=mx[moving][0],
                rhs_scale=mx[moving][1],
                start=start,
                stop=stop,
            )

        raw = {}
        wt = {}

        def load_v(g):
            raw["v", g] = sbuf("stage", [P, PACK * DH], BF16, STAGE_BUFS)
            nc.sync.dma_start(out=raw["v", g][:].rearrange("m (s d) -> m s d", s=PACK), in_=v_rows[:, g])

        def load_g(j):
            raw["g", j] = sbuf("stage", [P, H * DH], BF16, STAGE_BUFS)
            nc.sync.dma_start(out=raw["g", j][:], in_=g_rows[:, j])

        def load_pair(key, pair):
            raw[key, pair] = sbuf("pair", [P, PACK, 2 * DH], BF16, PAIR_BUFS)
            nc.sync.dma_start(out=raw[key, pair][:], in_=row_operand[key][:, :, 2 * DH * pair : 2 * DH * (pair + 1)])

        def load_w(g, h, rows):
            if rows.start == 0:
                wt[g, h] = sbuf("w", [P, PACK, PASS], F32, W_BUFS)
            nc.sync.dma_start(out=wt[g, h][:, rows, :], in_=w_rows[:, h, rows, PASS * g : PASS * (g + 1)])

        ident = sbuf("ident", [P, P], F32, 1)
        zeros = sbuf("zeros", [P, PASS], BF16, 1)
        grouped = {}

        def turn(key, half, engine):
            words = raw[key][:].bitcast(F32)
            bank = take_bank("turn")
            for i in range(PACK):
                run, u = 2 * half + i // 2, i % 2
                nc.tensor.transpose(
                    bank[:, i * P : (i + 1) * P], words[:, WORDS * run + u : WORDS * (run + 1) : 2], ident[:]
                )
            if half == 0:
                grouped[key] = sbuf("grouped", [P, PACK * PASS], BF16, GROUPED_BUFS)
            out_words = grouped[key][:].bitcast(F32)
            runs = slice(2 * half, 2 * half + 2)
            if key[0] == "g":
                dst = out_words.rearrange("x (h p u) -> x h p u", h=H, u=2)[:, runs]
                copy(engine, dst, bank[:].rearrange("x (h u p) -> x h p u", h=2, u=2))
            else:
                dst = out_words.rearrange("x (m s u) -> x m s u", s=PACK, u=2)[:, :, runs]
                copy(engine, dst, bank[:].rearrange("x (s u m) -> x m s u", s=2, u=2))
            give_bank("turn")

        def quantise_v(g):
            quantise(("v", g), grouped["v", g][:], E4M3, "v", HALVES)

        def quantise_g(j, pair):
            quantise(("g", j, pair), grouped["g", j][:, 2 * PASS * pair : 2 * PASS * (pair + 1)], E5M2, "g", 2 * PACK)

        def interleave(key, h, engines):
            grouped[key, h] = sbuf("grouped", [P, PACK * DH], BF16, GROUPED_BUFS)
            parts = 1 if engines[1] is gpsimd else 2
            cols = DH // parts
            for a in range(parts):
                first = DH * (h % 2) + cols * a
                src = raw[key, h // 2][:, :, first : first + cols]
                dst = grouped[key, h][:, PACK * cols * a : PACK * cols * (a + 1)]
                if engines[a] is gpsimd:
                    nc.gpsimd.tensor_scalar(
                        out=dst.rearrange("p (c j) -> p c j", j=PACK),
                        in0=src.rearrange("p j c -> p c j"),
                        scalar1=1.0,
                        scalar2=0.0,
                        op0=ALU.mult,
                        op1=ALU.add,
                    )
                else:
                    copy(
                        engines[a],
                        dst.rearrange("p (c i j) -> p c j i", i=4, j=PACK),
                        src.rearrange("p j (c i) -> p c j i", i=4),
                    )

        def quantise_rows(key, h):
            quantise((key, h), grouped[key, h][:], E4M3, key, H)

        def warm(count):
            bank = take_bank("warm")
            for i in range(count):
                nc.tensor.matmul(bank[:], lhsT=zeros[:, :P], rhs=zeros[:], start=True, stop=True)
            give_bank("warm")

        prod = {}
        r_turned = {}

        def dw_pass(g, j, h):
            mx_pass(take_bank(("dw", j, h)), (("g", j, h // 2), h % 2), ("v", g), True, True)

        def dw_pair(g, j, pair):
            dw_pass(g, j, 2 * pair)
            dw_pass(g, j, 2 * pair + 1)

        def product(g, j, h):
            if j == 0:
                prod[h] = sbuf("prod", [P, PACK, PASS], F32, H)
            nc.vector.scalar_tensor_tensor(
                out=prod[h][:, j, :],
                in0=held["dw", j, h][0][:],
                scalar=SCALE,
                in1=wt[g, h][:, j, :],
                op0=ALU.mult,
                op1=ALU.mult,
            )
            give_bank(("dw", j, h))

        def head_sum(j, half):
            bank = take_bank(("r", j)) if half == 0 else held["r", j][0]
            for b in (2 * half, 2 * half + 1):
                cols = slice(b * P, (b + 1) * P)
                for h in range(H):
                    nc.tensor.matmul(
                        bank[:, cols],
                        lhsT=prod[h][:, j, cols],
                        rhs=ident[:],
                        start=h == 0,
                        stop=h == H - 1,
                        is_transpose=True,
                    )

        def save_sum(j):
            r_turned[j] = sbuf("r_turned", [P, PASS], F32, 2)
            nc.scalar.copy(out=r_turned[j][:], in_=held["r", j][0][:])

        def turn_back(j):
            bank = take_bank(("r", j), held["r", j][1])
            for b in range(PACK):
                cols = slice(b * P, (b + 1) * P)
                nc.tensor.transpose(bank[:, cols], r_turned[j][:, cols], ident[:])

        ds_q = {}
        ds_t = {}
        r_readers = {}

        def times_r(g, h, j):
            nc.vector.tensor_tensor(out=wt[g, h][:, j, :], in0=held["r", j][0][:], in1=wt[g, h][:, j, :], op=ALU.mult)
            r_readers[g, j] = r_readers.get((g, j), 0) + 1
            if r_readers[g, j] == H:
                give_bank(("r", j))

        def make_ds(g, h):
            ds_q[h] = sbuf("ds_q", [P, PACK * PASS], BF16, DS_BUFS)
            words = ds_q[h][:].bitcast(F32)
            banks = [take_bank(("ds", h, jj)) for jj in range(2)]
            view = "p j (m u e) -> p u m j e"
            for u in range(2):
                nc.vector.tensor_tensor(
                    out=ds_q[h][:].rearrange("p (u e m j) -> p u m j e", u=2, e=2, j=PACK)[:, u],
                    in0=prod[h][:].rearrange(view, u=2, e=2)[:, u],
                    in1=wt[g, h][:].rearrange(view, u=2, e=2)[:, u],
                    op=ALU.subtract,
                )
                for jj in range(2):
                    for s in (2 * u, 2 * u + 1):
                        nc.tensor.transpose(
                            banks[jj][:, s * P : (s + 1) * P], words[:, WORDS * s + jj : WORDS * (s + 1) : 2], ident[:]
                        )

        def save_ds_t(h, rows, engine):
            if rows.start == 0:
                ds_t[h] = sbuf("ds_t", [P, PACK * PASS], BF16, DS_BUFS)
            jj = rows.start // 2
            src = held["ds", h, jj][0][:].bitcast(BF16).rearrange("m (s p e) -> m e p s", s=PACK, e=2)
            copy(
                engine,
                ds_t[h][:].rearrange("m (j p s) -> m j p s", j=PACK, s=PACK)[:, rows],
                src[:, rows.start - 2 * jj : rows.stop - 2 * jj],
            )
            if rows.stop == 2 * jj + 2:
                give_bank(("ds", h, jj))

        def quantise_ds(tiles, name, g, h, rows, bufs):
            count = rows.stop - rows.start
            key = (name, g, h, rows.start)
            quantise(key, tiles[h][:, PASS * rows.start : PASS * rows.stop], E5M2, "%s%d" % (name, count), bufs)
            for block in range(count):
                mx[name, g, h, "block", rows.start + block] = mx[key, block]

        ALL, LOW, HIGH = slice(0, 4), slice(0, 2), slice(2, 4)

        def quantise_ds_q(g, h):
            quantise_ds(ds_q, "ds_q", g, h, ALL, LATE_HEADS + 1)

        def grad_k(g, h, s):
            mx_pass(take_bank(("dk", g, h, s)), ("ds_q", g, h, "block", s), (Q, h), True, True)

        def grad_q(h, j):
            bank = take_bank(("dq", h, j))
            for g, key in enumerate((K0, K1)):
                mx_pass(bank, ("ds_t", g, h, "block", j), (key, h), g == 0, g == HALVES - 1)

        result = {}

        def save(key, rows, engine):
            h, i = key[-2:]
            if i % 2 == 0:
                result[key[0]] = sbuf("stage", [P, 2, DH], F32, STAGE_BUFS)
            copy(engine, result[key[0]][:, i % 2, :], held[key][0][:])
            give_bank(key)
            if i % 2 == 1:
                nc.sync.dma_start(out=rows[:, i - 1 : i + 1, DH * h : DH * (h + 1)], in_=result[key[0]][:])

        def save_alone(key, rows, engine, tag, bufs):
            h, i = key[-2:]
            tile = sbuf(tag, [P, 1, DH], F32, bufs)
            copy(engine, tile[:, 0, :], held[key][0][:])
            give_bank(key)
            nc.sync.dma_start(out=rows[:, i : i + 1, DH * h : DH * (h + 1)], in_=tile[:])

        def save_k(g, h, s):
            save(("dk", g, h, s), dk_rows[:, g], scalar)

        on_scalar = (scalar, scalar)
        on_gpsimd = (gpsimd, gpsimd)

        load_v(0)
        load_g(0)
        load_g(1)
        load_w(0, 0, LOW)
        load_w(0, 1, LOW)
        load_g(2)
        load_w(0, 2, LOW)
        load_g(3)
        load_w(0, 3, LOW)
        load_w(0, 0, HIGH)
        load_pair(Q, 0)
        for h in range(1, H):
            load_w(0, h, HIGH)
        load_pair(Q, 1)
        load_pair(K0, 0)
        load_pair(K1, 0)
        nc.vector.memset(zeros[:], 0.0)
        make_identity(nc, ident[:])

        warm(6)
        turn(("v", 0), 0, scalar)
        turn(("v", 0), 1, vector)
        warm(3)
        turn(("g", 0), 0, scalar)
        turn(("g", 0), 1, scalar)
        load_v(1)
        load_w(1, 0, ALL)
        load_w(1, 1, ALL)
        warm(3)
        quantise_v(0)
        quantise_g(0, 0)
        turn(("g", 1), 0, scalar)
        dw_pair(0, 0, 0)
        turn(("g", 1), 1, scalar)
        quantise_g(0, 1)
        product(0, 0, 0)
        quantise_g(1, 0)
        turn(("g", 2), 0, scalar)
        dw_pair(0, 0, 1)
        product(0, 0, 1)
        quantise_g(1, 1)
        turn(("g", 2), 1, scalar)
        dw_pair(0, 1, 0)
        product(0, 0, 2)
        quantise_g(2, 0)
        turn(("g", 3), 0, scalar)
        turn(("g", 3), 1, scalar)
        dw_pair(0, 1, 1)
        product(0, 1, 0)
        quantise_g(2, 1)
        product(0, 0, 3)
        product(0, 1, 1)
        head_sum(0, 0)
        head_sum(0, 1)
        save_sum(0)
        interleave(Q, 0, on_scalar)
        dw_pair(0, 2, 0)
        product(0, 1, 2)
        quantise_g(3, 0)
        product(0, 1, 3)
        quantise_g(3, 1)
        head_sum(1, 0)
        dw_pair(0, 2, 1)
        head_sum(1, 1)
        save_sum(1)
        interleave(Q, 1, on_scalar)
        product(0, 2, 0)
        product(0, 2, 1)
        dw_pair(0, 3, 0)
        turn_back(0)
        product(0, 2, 2)
        turn_back(1)
        product(0, 3, 0)
        dw_pair(0, 3, 1)
        product(0, 2, 3)
        product(0, 3, 1)
        times_r(0, 0, 0)
        product(0, 3, 2)
        product(0, 3, 3)
        head_sum(2, 0)
        warm(2)
        head_sum(2, 1)
        save_sum(2)
        head_sum(3, 0)
        head_sum(3, 1)
        load_pair(K0, 1)
        turn_back(2)
        save_sum(3)
        turn_back(3)
        for h, j in ((0, 1), (1, 0), (1, 1)):
            times_r(0, h, j)
        quantise_rows(Q, 0)
        interleave(Q, 2, on_scalar)
        for h, j in ((2, 0), (2, 1), (0, 2), (1, 2)):
            times_r(0, h, j)
        quantise_rows(Q, 1)
        interleave(Q, 3, on_scalar)
        load_pair(K1, 1)
        times_r(0, 0, 3)
        times_r(0, 1, 3)

        def first_ds(h):
            make_ds(0, h)
            if h + 2 < H:
                load_w(1, h + 2, ALL)
                quantise_rows(Q, h + 2)
            if h == 0:
                interleave(K0, 0, on_scalar)
            else:
                quantise_ds(ds_t, "ds_t", 0, h - 1, ALL, H)
            save_ds_t(h, LOW, scalar)
            save_ds_t(h, HIGH, scalar)

        def grad_k_head(g, h):
            for s in range(PACK):
                grad_k(g, h, s)
                save_k(g, h, s)

        first_ds(0)
        quantise_ds_q(0, 0)
        grad_k_head(0, 0)
        first_ds(1)
        times_r(0, 2, 2)
        quantise_ds_q(0, 1)
        times_r(0, 2, 3)
        quantise_rows(K0, 0)
        turn(("v", 1), 0, scalar)
        turn(("v", 1), 1, scalar)
        grad_k_head(0, 1)
        first_ds(2)
        times_r(0, 3, 0)
        quantise_ds_q(0, 2)
        for j in range(1, PACK):
            times_r(0, 3, j)
        quantise_v(1)
        for h in range(H):
            dw_pass(1, 0, h)
        interleave(K1, 0, on_scalar)
        first_ds(3)

        late = [(h, s) for h in range(H - LATE_HEADS, H) for s in range(PACK)]
        for j in range(PACK):
            if j > 0:
                head_sum(j - 1, 0)
            if j > 1:
                turn_back(j - 2)
            for h in range(H):
                product(1, j, h)
                if j + 1 < PACK:
                    dw_pass(1, j + 1, h)
                elif h + 1 < H:
                    grad_k(0, *late[h])
                if j == 0 and h == 0:
                    quantise_ds_q(0, H - 1)
                if j > 0 and h == 1:
                    head_sum(j - 1, 1)
                    save_sum(j - 1)
            if j == 0:
                quantise_rows(K1, 0)
                interleave(K0, 1, on_scalar)
            if j == 1:
                quantise_ds(ds_t, "ds_t", 0, H - 1, ALL, H)
                interleave(K1, 1, on_scalar)
            if j == 2:
                quantise_rows(K0, 1)
                interleave(K0, 2, on_scalar)
                interleave(K1, 2, on_gpsimd)
        save_k(0, *late[0])
        save_k(0, *late[1])
        head_sum(3, 0)
        head_sum(3, 1)
        turn_back(2)
        save_sum(3)
        grad_k(0, *late[3])
        turn_back(3)
        grad_k(0, *late[4])
        for i in range(2, len(late)):
            save_k(0, *late[i])
            if i + 3 < len(late):
                grad_k(0, *late[i + 3])
        times_r(1, 0, 0)
        times_r(1, 0, 1)
        quantise_rows(K0, 2)
        quantise_rows(K1, 1)
        interleave(K0, 3, on_gpsimd)
        interleave(K1, 3, (gpsimd, scalar))
        for h, j in ((1, 0), (1, 1), (0, 2), (1, 2), (2, 0), (0, 3)):
            times_r(1, h, j)

        left = (((1, 3), (2, 1), (3, 0), (3, 1)), ((2, 2), (2, 3)), ((3, 2), (3, 3)))
        k_left = ((K1, 2), (K0, 3), (K1, 3))
        for h in range(H - 1):
            make_ds(1, h)
            save_ds_t(h, LOW, scalar)
            times_r(1, *left[h][0])
            quantise_ds_q(1, h)
            save_ds_t(h, HIGH, vector if h == H - 2 else scalar)
            grad_k_head(1, h)
            for pair in left[h][1:]:
                times_r(1, *pair)
            quantise_rows(*k_left[h])
            quantise_ds(ds_t, "ds_t", 1, h, LOW, PACK)
            quantise_ds(ds_t, "ds_t", 1, h, HIGH, PACK)
            for j in range(PACK):
                grad_q(h, j)
                save(("dq", h, j), dq_rows, scalar)

        h = H - 1
        make_ds(1, h)
        quantise_ds(ds_q, "ds_q", 1, h, LOW, 2)
        quantise_ds(ds_q, "ds_q", 1, h, HIGH, 2)
        for s in range(PACK):
            grad_k(1, h, s)
            save_alone(("dk", 1, h, s), dk_rows[:, 1], scalar, "pair", PAIR_BUFS)
        save_ds_t(h, slice(0, 1), vector)
        for j in range(PACK):
            if j + 1 < PACK:
                save_ds_t(h, slice(j + 1, j + 2), vector)
            quantise_ds(ds_t, "ds_t", 1, h, slice(j, j + 1), PACK)
            grad_q(h, j)
        for j in range(PACK):
            save_alone(("dq", h, j), dq_rows, vector if j == PACK - 1 else scalar, "w", W_BUFS)
